import numpy as np
import ml_dtypes


def mxq(x, axis, fmt="e4m3"):
    dtype, down = {"e4m3": (ml_dtypes.float8_e4m3fn, 7), "e5m2": (ml_dtypes.float8_e5m2, 14)}[fmt]
    v = np.moveaxis(np.asarray(x, np.float32).astype(ml_dtypes.bfloat16).astype(np.float64), axis, -1)
    blocks = v.reshape(v.shape[:-1] + (-1, 32))
    amax = np.abs(blocks).max(-1, keepdims=True)
    byte = np.maximum(np.where(amax > 0, np.frexp(amax)[1] - 1 + 127, 0) - down, 1)
    scale = np.exp2(byte - 127.0)
    codes = (blocks / scale).astype(np.float32).astype(dtype).astype(np.float64)
    return np.moveaxis((codes * scale).reshape(v.shape), -1, axis)


WIDE = False


def mx_kscale(k):
    if not WIDE:
        return np.ones(k)
    levels = np.array([10, -10, 5, -5, 0])
    a = np.random.permutation(np.resize(levels, k // 512 * 4)).reshape(k // 512, 4)
    idx = np.arange(k)
    return np.exp2(a[idx // 512, idx % 128 // 32])


BF16 = ml_dtypes.bfloat16


def bf(x):
    return np.asarray(x, np.float32).astype(BF16)


def f64(x):
    return np.asarray(x).astype(np.float64)


B, DIN, H1, H2, N, I, K, O = 768, 2048, 1024, 512, 32, 16, 128, 8
KO = K * O
SQ_EPS = 1e-8


def squash(t):
    sq = np.sum(t * t, axis=-1, keepdims=True)
    return (sq / (1.0 + sq)) * t / np.sqrt(sq + SQ_EPS)


def setup_inputs():
    amp = np.exp(0.8 * np.random.standard_normal((B, K, 1)))
    t = np.repeat(np.asarray(mx_kscale(KO))[::O], O)
    h = np.exp2(np.round(np.log2(t) / 2))
    c = h / h.max()
    d = np.where(c < 1.0, 0.0625, 1.0)
    return {"s": bf(np.random.standard_normal((B, K, O)) * amp * 1.4 / np.sqrt(O) * c.reshape(K, O)),
            "Wc": bf(np.random.standard_normal((KO, K)) * 6.0 / np.sqrt(KO) * (d / (c * c))[:, None]),
            "bc": bf(np.random.standard_normal(K) * 0.2)}


def reference(s, Wc, bc):
    v = squash(f64(s)).reshape(B, KO)
    return (mxq(v, 1, "e4m3") @ mxq(f64(Wc), 0, "e4m3")) + f64(bc)

@@ -1,0 +1,186 @@
+from contextlib import ExitStack
+
+import concourse.mybir as mybir
+from concourse.masks import make_identity
+
+F32 = mybir.dt.float32
+BF16 = mybir.dt.bfloat16
+U32 = mybir.dt.uint32
+U8 = mybir.dt.uint8
+FP8X4 = mybir.dt.float8_e4m3fn_x4
+ACT = mybir.ActivationFunctionType
+ALU = mybir.AluOpType
+
+P = 128
+PACK = 4
+K_PASS = P * PACK
+
+BATCH = 768
+CAPS = 128
+CAP_LEN = 8
+K_TOTAL = CAPS * CAP_LEN
+N_OUT = 128
+SQ_EPS = 1e-8
+
+B_TILES = BATCH // P
+PASSES = K_TOTAL // K_PASS
+CAPS_PER_PASS = CAPS // PASSES
+PARTS_PER_CAP = CAP_LEN // PACK
+WORD = 2
+WORDS_PER_PART = PACK // WORD
+
+FLOPS = 2 * BATCH * K_TOTAL * N_OUT
+
+
+def quantise_weights(nc, pools, Wc):
+    w_raw = pools["keep"].tile([P, PASSES, PACK, N_OUT], BF16)
+    nc.sync.dma_start(out=w_raw[:], in_=Wc.rearrange("(g p t) n -> p g t n", g=PASSES, t=PACK))
+    w_grouped = pools["keep"].tile([P, PASSES, N_OUT, PACK], BF16, align_bytes=64)
+    nc.vector.tensor_copy(out=w_grouped[:], in_=w_raw[:].rearrange("p g t n -> p g n t"))
+    w_codes = pools["keep"].tile([P, PASSES, N_OUT], U32, align_bytes=64)
+    w_scales = pools["keep"].tile([P, PASSES, N_OUT], U8, align_bytes=64)
+    nc.vector.quantize_mx(
+        out=w_codes[:].rearrange("p g n -> p (g n)").bitcast(FP8X4),
+        scales=w_scales[:].rearrange("p g n -> p (g n)"),
+        in_=w_grouped[:].rearrange("p g n t -> p (g n t)"),
+    )
+    return w_codes, w_scales
+
+
+def squash_factor(nc, pools, consts, s_tile):
+    small = pools["small"]
+    squares = pools["work"].tile([P, K_TOTAL], F32)
+    nc.scalar.activation(out=squares[:], in_=s_tile[:], func=ACT.Square)
+    q = small.tile([P, CAPS], F32)
+    nc.vector.tensor_reduce(
+        out=q[:],
+        in_=squares[:].rearrange("b (j o) -> b j o", o=CAP_LEN),
+        axis=mybir.AxisListType.X,
+        op=ALU.add,
+    )
+    q_eps = small.tile([P, CAPS], F32)
+    nc.scalar.activation(out=q_eps[:], in_=q[:], func=ACT.Identity, bias=consts["eps"])
+    inv_len = small.tile([P, CAPS], F32)
+    nc.scalar.activation(out=inv_len[:], in_=q_eps[:], func=ACT.Abs_reciprocal_sqrt)
+    inv_root = small.tile([P, CAPS], F32)
+    nc.scalar.activation(out=inv_root[:], in_=q[:], func=ACT.Abs_reciprocal_sqrt, bias=consts["one"])
+    inv_one_plus_q = small.tile([P, CAPS], F32)
+    nc.scalar.activation(out=inv_one_plus_q[:], in_=inv_root[:], func=ACT.Square)
+    h = small.tile([P, CAPS], F32)
+    nc.gpsimd.tensor_tensor(out=h[:], in0=inv_len[:], in1=inv_one_plus_q[:], op=ALU.mult)
+    qh = small.tile([P, CAPS], F32)
+    nc.gpsimd.tensor_tensor(out=qh[:], in0=q[:], in1=h[:], op=ALU.mult)
+    one_plus_q_h = small.tile([P, CAPS], F32)
+    nc.gpsimd.tensor_tensor(out=one_plus_q_h[:], in0=qh[:], in1=h[:], op=ALU.add)
+    one_plus_q_h_sq = small.tile([P, CAPS], F32)
+    nc.scalar.activation(out=one_plus_q_h_sq[:], in_=one_plus_q_h[:], func=ACT.Square)
+    x_h_h = small.tile([P, CAPS], F32)
+    nc.gpsimd.tensor_tensor(out=x_h_h[:], in0=q_eps[:], in1=one_plus_q_h_sq[:], op=ALU.mult)
+    step = small.tile([P, CAPS], F32)
+    nc.scalar.activation(
+        out=step[:], in_=x_h_h[:], func=ACT.Identity, scale=-0.5, bias=consts["three_halves"]
+    )
+    doubled = [P, CAPS, PARTS_PER_CAP]
+    factor = small.tile(doubled, F32)
+    nc.gpsimd.tensor_tensor(
+        out=factor[:],
+        in0=qh[:].unsqueeze(2).to_broadcast(doubled),
+        in1=step[:].unsqueeze(2).to_broadcast(doubled),
+        op=ALU.mult,
+    )
+    return factor
+
+
+def tile_capsulenetwork_pc_s_kernel(tc, s, Wc, bc, out):
+    nc = tc.nc
+    s_rows = s.rearrange("(i b) j o -> i b (j o)", b=P)
+    out_rows = out.rearrange("(i b) n -> i b n", b=P)
+
+    with ExitStack() as ctx:
+        pools = {
+            "keep": ctx.enter_context(tc.tile_pool(name="keep", bufs=1)),
+            "s": ctx.enter_context(tc.tile_pool(name="s", bufs=B_TILES)),
+            "work": ctx.enter_context(tc.tile_pool(name="work", bufs=B_TILES)),
+            "small": ctx.enter_context(tc.tile_pool(name="small", bufs=B_TILES)),
+        }
+        psum_s = ctx.enter_context(tc.psum_pool(name="psum_s", bufs=4))
+        psum_f = ctx.enter_context(tc.psum_pool(name="psum_f", bufs=2))
+        psum_o = ctx.enter_context(tc.psum_pool(name="psum_o", bufs=2))
+
+        const_cols = pools["keep"].tile([P, 3], F32)
+        nc.vector.memset(const_cols[:, 0:1], SQ_EPS)
+        nc.vector.memset(const_cols[:, 1:2], 1.0)
+        nc.vector.memset(const_cols[:, 2:3], 1.5)
+        consts = {
+            "eps": const_cols[:, 0:1],
+            "one": const_cols[:, 1:2],
+            "three_halves": const_cols[:, 2:3],
+        }
+        table_warm = pools["keep"].tile([P, 1], F32)
+        nc.scalar.activation(out=table_warm[:], in_=consts["one"], func=ACT.Abs_reciprocal_sqrt)
+        ident = pools["keep"].tile([P, P], F32)
+        make_identity(nc, ident[:])
+
+        s_tiles = []
+        for i in range(B_TILES):
+            s_tile = pools["s"].tile([P, K_TOTAL], BF16, name="s_tile")
+            nc.sync.dma_start(out=s_tile[:], in_=s_rows[i])
+            s_tiles.append(s_tile)
+            if i == 0:
+                w_codes, w_scales = quantise_weights(nc, pools, Wc)
+        bias = pools["keep"].tile([P, N_OUT], BF16)
+        nc.sync.dma_start(out=bias[:], in_=bc.partition_broadcast(P))
+
+        for i in range(B_TILES):
+            s_tile = s_tiles[i]
+            factor = squash_factor(nc, pools, consts, s_tile)
+
+            s_words = s_tile[:].bitcast(F32).rearrange(
+                "b (g p u) -> b g u p", g=PASSES, u=WORDS_PER_PART
+            )
+            sT = psum_s.tile([P, WORDS_PER_PART, PASSES, P], F32)
+            for g in range(PASSES):
+                for u in range(WORDS_PER_PART):
+                    nc.tensor.transpose(sT[:, u, g, :], s_words[:, g, u, :], ident[:])
+
+            fT_psum = psum_f.tile([P, PASSES, P], F32)
+            for g in range(PASSES):
+                caps = slice(g * CAPS_PER_PASS, (g + 1) * CAPS_PER_PASS)
+                nc.tensor.transpose(
+                    fT_psum[:, g, :], factor[:, caps, :].rearrange("b j d -> b (j d)"), ident[:]
+                )
+            fT = pools["small"].tile([P, PASSES * P], F32)
+            nc.scalar.copy(out=fT[:], in_=fT_psum[:].rearrange("p g b -> p (g b)"))
+
+            v_grouped = pools["work"].tile([P, PASSES * P, WORDS_PER_PART, WORD], BF16, align_bytes=64)
+            nc.vector.tensor_tensor(
+                out=v_grouped[:],
+                in0=sT[:].rearrange("p u g b -> p u (g b)").bitcast(BF16).rearrange(
+                    "p u (n e) -> p n u e", e=WORD
+                ),
+                in1=fT[:].unsqueeze(2).unsqueeze(3).to_broadcast([P, PASSES * P, WORDS_PER_PART, WORD]),
+                op=ALU.mult,
+            )
+            v_codes = pools["work"].tile([P, PASSES * P], U32, align_bytes=64)
+            v_scales = pools["work"].tile([P, PASSES * P], U8, align_bytes=64)
+            nc.vector.quantize_mx(
+                out=v_codes[:].bitcast(FP8X4),
+                scales=v_scales[:],
+                in_=v_grouped[:].rearrange("p n u e -> p (n u e)"),
+            )
+
+            acc = psum_o.tile([P, N_OUT], F32)
+            for g in range(PASSES):
+                rows = slice(g * P, (g + 1) * P)
+                nc.tensor.matmul_mx(
+                    out=acc[:],
+                    lhsT=v_codes[:, rows].bitcast(FP8X4),
+                    lhsT_scale=v_scales[:, rows],
+                    rhs=w_codes[:, g, :].bitcast(FP8X4),
+                    rhs_scale=w_scales[:, g, :],
+                    start=(g == 0),
+                    stop=(g == PASSES - 1),
+                )
+            result = pools["work"].tile([P, N_OUT], F32)
+            nc.vector.tensor_tensor(out=result[:], in0=acc[:], in1=bias[:], op=ALU.add)
+            nc.sync.dma_start(out=out_rows[i], in_=result[:])

@@ -21,6 +21,7 @@ CAP_LEN = 8
 K_TOTAL = CAPS * CAP_LEN
 N_OUT = 128
 SQ_EPS = 1e-8
+NEWTON_SCALE = -0.5
 
 B_TILES = BATCH // P
 PASSES = K_TOTAL // K_PASS
@@ -29,66 +30,13 @@ PARTS_PER_CAP = CAP_LEN // PACK
 WORD = 2
 WORDS_PER_PART = PACK // WORD
 
+LAG_GUESS = 2
+LAG_NEWTON = 3
+LAG_MULTIPLY = 4
+LAG_STORE = 5
+S_BANKS = LAG_MULTIPLY
+
 FLOPS = 2 * BATCH * K_TOTAL * N_OUT
-
-
-def quantise_weights(nc, pools, Wc):
-    w_raw = pools["keep"].tile([P, PASSES, PACK, N_OUT], BF16)
-    nc.sync.dma_start(out=w_raw[:], in_=Wc.rearrange("(g p t) n -> p g t n", g=PASSES, t=PACK))
-    w_grouped = pools["keep"].tile([P, PASSES, N_OUT, PACK], BF16, align_bytes=64)
-    nc.vector.tensor_copy(out=w_grouped[:], in_=w_raw[:].rearrange("p g t n -> p g n t"))
-    w_codes = pools["keep"].tile([P, PASSES, N_OUT], U32, align_bytes=64)
-    w_scales = pools["keep"].tile([P, PASSES, N_OUT], U8, align_bytes=64)
-    nc.vector.quantize_mx(
-        out=w_codes[:].rearrange("p g n -> p (g n)").bitcast(FP8X4),
-        scales=w_scales[:].rearrange("p g n -> p (g n)"),
-        in_=w_grouped[:].rearrange("p g n t -> p (g n t)"),
-    )
-    return w_codes, w_scales
-
-
-def squash_factor(nc, pools, consts, s_tile):
-    small = pools["small"]
-    squares = pools["work"].tile([P, K_TOTAL], F32)
-    nc.scalar.activation(out=squares[:], in_=s_tile[:], func=ACT.Square)
-    q = small.tile([P, CAPS], F32)
-    nc.vector.tensor_reduce(
-        out=q[:],
-        in_=squares[:].rearrange("b (j o) -> b j o", o=CAP_LEN),
-        axis=mybir.AxisListType.X,
-        op=ALU.add,
-    )
-    q_eps = small.tile([P, CAPS], F32)
-    nc.scalar.activation(out=q_eps[:], in_=q[:], func=ACT.Identity, bias=consts["eps"])
-    inv_len = small.tile([P, CAPS], F32)
-    nc.scalar.activation(out=inv_len[:], in_=q_eps[:], func=ACT.Abs_reciprocal_sqrt)
-    inv_root = small.tile([P, CAPS], F32)
-    nc.scalar.activation(out=inv_root[:], in_=q[:], func=ACT.Abs_reciprocal_sqrt, bias=consts["one"])
-    inv_one_plus_q = small.tile([P, CAPS], F32)
-    nc.scalar.activation(out=inv_one_plus_q[:], in_=inv_root[:], func=ACT.Square)
-    h = small.tile([P, CAPS], F32)
-    nc.gpsimd.tensor_tensor(out=h[:], in0=inv_len[:], in1=inv_one_plus_q[:], op=ALU.mult)
-    qh = small.tile([P, CAPS], F32)
-    nc.gpsimd.tensor_tensor(out=qh[:], in0=q[:], in1=h[:], op=ALU.mult)
-    one_plus_q_h = small.tile([P, CAPS], F32)
-    nc.gpsimd.tensor_tensor(out=one_plus_q_h[:], in0=qh[:], in1=h[:], op=ALU.add)
-    one_plus_q_h_sq = small.tile([P, CAPS], F32)
-    nc.scalar.activation(out=one_plus_q_h_sq[:], in_=one_plus_q_h[:], func=ACT.Square)
-    x_h_h = small.tile([P, CAPS], F32)
-    nc.gpsimd.tensor_tensor(out=x_h_h[:], in0=q_eps[:], in1=one_plus_q_h_sq[:], op=ALU.mult)
-    step = small.tile([P, CAPS], F32)
-    nc.scalar.activation(
-        out=step[:], in_=x_h_h[:], func=ACT.Identity, scale=-0.5, bias=consts["three_halves"]
-    )
-    doubled = [P, CAPS, PARTS_PER_CAP]
-    factor = small.tile(doubled, F32)
-    nc.gpsimd.tensor_tensor(
-        out=factor[:],
-        in0=qh[:].unsqueeze(2).to_broadcast(doubled),
-        in1=step[:].unsqueeze(2).to_broadcast(doubled),
-        op=ALU.mult,
-    )
-    return factor
 
 
 def tile_capsulenetwork_pc_s_kernel(tc, s, Wc, bc, out):
@@ -97,78 +45,137 @@ def tile_capsulenetwork_pc_s_kernel(tc, s, Wc, bc, out):
     out_rows = out.rearrange("(i b) n -> i b n", b=P)
 
     with ExitStack() as ctx:
-        pools = {
-            "keep": ctx.enter_context(tc.tile_pool(name="keep", bufs=1)),
-            "s": ctx.enter_context(tc.tile_pool(name="s", bufs=B_TILES)),
-            "work": ctx.enter_context(tc.tile_pool(name="work", bufs=B_TILES)),
-            "small": ctx.enter_context(tc.tile_pool(name="small", bufs=B_TILES)),
-        }
-        psum_s = ctx.enter_context(tc.psum_pool(name="psum_s", bufs=4))
+        ctx.enter_context(tc.manual_schedule())
+        keep = ctx.enter_context(tc.tile_pool(name="keep", bufs=1))
+        per_tile = ctx.enter_context(tc.tile_pool(name="per_tile", bufs=B_TILES))
+        psum_s = ctx.enter_context(tc.psum_pool(name="psum_s", bufs=S_BANKS))
         psum_f = ctx.enter_context(tc.psum_pool(name="psum_f", bufs=2))
         psum_o = ctx.enter_context(tc.psum_pool(name="psum_o", bufs=2))
 
-        const_cols = pools["keep"].tile([P, 3], F32)
+        const_cols = keep.tile([P, 2], F32)
         nc.vector.memset(const_cols[:, 0:1], SQ_EPS)
         nc.vector.memset(const_cols[:, 1:2], 1.0)
-        nc.vector.memset(const_cols[:, 2:3], 1.5)
-        consts = {
-            "eps": const_cols[:, 0:1],
-            "one": const_cols[:, 1:2],
-            "three_halves": const_cols[:, 2:3],
-        }
-        table_warm = pools["keep"].tile([P, 1], F32)
-        nc.scalar.activation(out=table_warm[:], in_=consts["one"], func=ACT.Abs_reciprocal_sqrt)
-        ident = pools["keep"].tile([P, P], F32)
+        eps_col = const_cols[:, 0:1]
+        one_col = const_cols[:, 1:2]
+        table_warm = keep.tile([P, 1], F32)
+        nc.scalar.activation(out=table_warm[:], in_=one_col, func=ACT.Abs_reciprocal_sqrt)
+        ident = keep.tile([P, P], F32)
         make_identity(nc, ident[:])
 
         s_tiles = []
         for i in range(B_TILES):
-            s_tile = pools["s"].tile([P, K_TOTAL], BF16, name="s_tile")
-            nc.sync.dma_start(out=s_tile[:], in_=s_rows[i])
+            s_tile = per_tile.tile([P, K_TOTAL], BF16)
             s_tiles.append(s_tile)
-            if i == 0:
-                w_codes, w_scales = quantise_weights(nc, pools, Wc)
-        bias = pools["keep"].tile([P, N_OUT], BF16)
+        w_raw = keep.tile([P, PASSES, PACK, N_OUT], BF16)
+        bias = keep.tile([P, N_OUT], BF16)
+        nc.sync.dma_start(out=s_tiles[0][:], in_=s_rows[0])
+        nc.sync.dma_start(out=w_raw[:], in_=Wc.rearrange("(g p t) n -> p g t n", g=PASSES, t=PACK))
+        for i in range(1, B_TILES):
+            nc.sync.dma_start(out=s_tiles[i][:], in_=s_rows[i])
         nc.sync.dma_start(out=bias[:], in_=bc.partition_broadcast(P))
 
-        for i in range(B_TILES):
-            s_tile = s_tiles[i]
-            factor = squash_factor(nc, pools, consts, s_tile)
+        w_grouped = keep.tile([P, PASSES, N_OUT, PACK], BF16, align_bytes=64)
+        nc.vector.tensor_copy(out=w_grouped[:], in_=w_raw[:].rearrange("p g t n -> p g n t"))
+        w_codes = keep.tile([P, PASSES, N_OUT], U32, align_bytes=64)
+        w_scales = keep.tile([P, PASSES, N_OUT], U8, align_bytes=64)
+        nc.vector.quantize_mx(
+            out=w_codes[:].rearrange("p g n -> p (g n)").bitcast(FP8X4),
+            scales=w_scales[:].rearrange("p g n -> p (g n)"),
+            in_=w_grouped[:].rearrange("p g n t -> p (g n t)"),
+        )
 
-            s_words = s_tile[:].bitcast(F32).rearrange(
-                "b (g p u) -> b g u p", g=PASSES, u=WORDS_PER_PART
+        q_of, qh_of, one_plus_q_h_of, fT_psum_of, sT_of, acc_of = {}, {}, {}, {}, {}, {}
+
+        def sum_squares(i):
+            squares = per_tile.tile([P, K_TOTAL], F32)
+            nc.scalar.activation(out=squares[:], in_=s_tiles[i][:], func=ACT.Square)
+            q = per_tile.tile([P, CAPS], F32)
+            nc.vector.tensor_reduce(
+                out=q[:],
+                in_=squares[:].rearrange("b (j o) -> b j o", o=CAP_LEN),
+                axis=mybir.AxisListType.X,
+                op=ALU.add,
             )
-            sT = psum_s.tile([P, WORDS_PER_PART, PASSES, P], F32)
-            for g in range(PASSES):
-                for u in range(WORDS_PER_PART):
-                    nc.tensor.transpose(sT[:, u, g, :], s_words[:, g, u, :], ident[:])
+            q_of[i] = q
 
+        def first_guess(i):
+            q = q_of[i]
+            inv_len = per_tile.tile([P, CAPS], F32)
+            nc.scalar.activation(out=inv_len[:], in_=q[:], func=ACT.Abs_reciprocal_sqrt, bias=eps_col)
+            inv_root = per_tile.tile([P, CAPS], F32)
+            nc.scalar.activation(out=inv_root[:], in_=q[:], func=ACT.Abs_reciprocal_sqrt, bias=one_col)
+            inv_one_plus_q = per_tile.tile([P, CAPS], F32)
+            nc.scalar.activation(out=inv_one_plus_q[:], in_=inv_root[:], func=ACT.Square)
+            h = per_tile.tile([P, CAPS], F32)
+            nc.gpsimd.tensor_tensor(out=h[:], in0=inv_len[:], in1=inv_one_plus_q[:], op=ALU.mult)
+            qh = per_tile.tile([P, CAPS], F32)
+            nc.gpsimd.tensor_tensor(out=qh[:], in0=q[:], in1=h[:], op=ALU.mult)
+            one_plus_q_h = per_tile.tile([P, CAPS], F32)
+            nc.gpsimd.tensor_tensor(out=one_plus_q_h[:], in0=qh[:], in1=h[:], op=ALU.add)
+            qh_of[i], one_plus_q_h_of[i] = qh, one_plus_q_h
+
+        def newton_step(i):
+            one_plus_q_h_sq = per_tile.tile([P, CAPS], F32)
+            nc.scalar.activation(out=one_plus_q_h_sq[:], in_=one_plus_q_h_of[i][:], func=ACT.Square)
+            x_h_h = per_tile.tile([P, CAPS], F32)
+            nc.vector.scalar_tensor_tensor(
+                out=x_h_h[:],
+                in0=q_of[i][:],
+                scalar=SQ_EPS,
+                in1=one_plus_q_h_sq[:],
+                op0=ALU.add,
+                op1=ALU.mult,
+            )
+            doubled = [P, CAPS, PARTS_PER_CAP]
+            factor = per_tile.tile(doubled, F32)
+            nc.vector.scalar_tensor_tensor(
+                out=factor[:],
+                in0=x_h_h[:].unsqueeze(2).to_broadcast(doubled),
+                scalar=-3.0,
+                in1=qh_of[i][:].unsqueeze(2).to_broadcast(doubled),
+                op0=ALU.add,
+                op1=ALU.mult,
+            )
             fT_psum = psum_f.tile([P, PASSES, P], F32)
             for g in range(PASSES):
                 caps = slice(g * CAPS_PER_PASS, (g + 1) * CAPS_PER_PASS)
                 nc.tensor.transpose(
                     fT_psum[:, g, :], factor[:, caps, :].rearrange("b j d -> b (j d)"), ident[:]
                 )
-            fT = pools["small"].tile([P, PASSES * P], F32)
-            nc.scalar.copy(out=fT[:], in_=fT_psum[:].rearrange("p g b -> p (g b)"))
+            fT_psum_of[i] = fT_psum
 
-            v_grouped = pools["work"].tile([P, PASSES * P, WORDS_PER_PART, WORD], BF16, align_bytes=64)
+        def transpose_s(i):
+            s_words = s_tiles[i][:].bitcast(F32).rearrange(
+                "b (g p u) -> b g u p", g=PASSES, u=WORDS_PER_PART
+            )
+            sT = psum_s.tile([P, WORDS_PER_PART, PASSES, P], F32)
+            for g in range(PASSES):
+                for u in range(WORDS_PER_PART):
+                    nc.tensor.transpose(sT[:, u, g, :], s_words[:, g, u, :], ident[:])
+            sT_of[i] = sT
+
+        def multiply(i):
+            fT = per_tile.tile([P, PASSES * P], F32)
+            nc.scalar.mul(
+                out=fT[:], in_=fT_psum_of[i][:].rearrange("p g b -> p (g b)"), mul=NEWTON_SCALE
+            )
+            grouped = [P, PASSES * P, WORDS_PER_PART, WORD]
+            v_grouped = per_tile.tile(grouped, BF16, align_bytes=64)
             nc.vector.tensor_tensor(
                 out=v_grouped[:],
-                in0=sT[:].rearrange("p u g b -> p u (g b)").bitcast(BF16).rearrange(
+                in0=sT_of[i][:].rearrange("p u g b -> p u (g b)").bitcast(BF16).rearrange(
                     "p u (n e) -> p n u e", e=WORD
                 ),
-                in1=fT[:].unsqueeze(2).unsqueeze(3).to_broadcast([P, PASSES * P, WORDS_PER_PART, WORD]),
+                in1=fT[:].unsqueeze(2).unsqueeze(3).to_broadcast(grouped),
                 op=ALU.mult,
             )
-            v_codes = pools["work"].tile([P, PASSES * P], U32, align_bytes=64)
-            v_scales = pools["work"].tile([P, PASSES * P], U8, align_bytes=64)
+            v_codes = per_tile.tile([P, PASSES * P], U32, align_bytes=64)
+            v_scales = per_tile.tile([P, PASSES * P], U8, align_bytes=64)
             nc.vector.quantize_mx(
                 out=v_codes[:].bitcast(FP8X4),
                 scales=v_scales[:],
                 in_=v_grouped[:].rearrange("p n u e -> p (n u e)"),
             )
-
             acc = psum_o.tile([P, N_OUT], F32)
             for g in range(PASSES):
                 rows = slice(g * P, (g + 1) * P)
@@ -181,6 +188,26 @@ def tile_capsulenetwork_pc_s_kernel(tc, s, Wc, bc, out):
                     start=(g == 0),
                     stop=(g == PASSES - 1),
                 )
-            result = pools["work"].tile([P, N_OUT], F32)
-            nc.vector.tensor_tensor(out=result[:], in0=acc[:], in1=bias[:], op=ALU.add)
+            acc_of[i] = acc
+
+        def add_bias_and_store(i):
+            result = per_tile.tile([P, N_OUT], F32)
+            nc.vector.tensor_tensor(out=result[:], in0=acc_of[i][:], in1=bias[:], op=ALU.add)
             nc.sync.dma_start(out=out_rows[i], in_=result[:])
+
+        def is_tile(i):
+            return 0 <= i < B_TILES
+
+        for step in range(B_TILES + LAG_STORE):
+            if is_tile(step):
+                sum_squares(step)
+            if is_tile(step - LAG_GUESS):
+                first_guess(step - LAG_GUESS)
+            if is_tile(step - LAG_NEWTON):
+                newton_step(step - LAG_NEWTON)
+            if is_tile(step - LAG_MULTIPLY):
+                multiply(step - LAG_MULTIPLY)
+            if is_tile(step):
+                transpose_s(step)
+            if is_tile(step - LAG_STORE):
+                add_bias_and_store(step - LAG_STORE)

@@ -33,7 +33,8 @@ WORDS_PER_PART = PACK // WORD
 LAG_GUESS = 2
 LAG_NEWTON = 3
 LAG_MULTIPLY = 4
-LAG_STORE = 5
+LAG_QUANTISE = 5
+LAG_STORE = 6
 S_BANKS = LAG_MULTIPLY
 
 FLOPS = 2 * BATCH * K_TOTAL * N_OUT
@@ -84,7 +85,8 @@ def tile_capsulenetwork_pc_s_kernel(tc, s, Wc, bc, out):
             in_=w_grouped[:].rearrange("p g n t -> p (g n t)"),
         )
 
-        q_of, qh_of, one_plus_q_h_of, fT_psum_of, sT_of, acc_of = {}, {}, {}, {}, {}, {}
+        q_of, qh_of, one_plus_q_h_of, x_h_h_of = {}, {}, {}, {}
+        fT_psum_of, sT_of, v_grouped_of, acc_of = {}, {}, {}, {}
 
         def sum_squares(i):
             squares = per_tile.tile([P, K_TOTAL], F32)
@@ -100,10 +102,10 @@ def tile_capsulenetwork_pc_s_kernel(tc, s, Wc, bc, out):
 
         def first_guess(i):
             q = q_of[i]
-            inv_len = per_tile.tile([P, CAPS], F32)
-            nc.scalar.activation(out=inv_len[:], in_=q[:], func=ACT.Abs_reciprocal_sqrt, bias=eps_col)
             inv_root = per_tile.tile([P, CAPS], F32)
             nc.scalar.activation(out=inv_root[:], in_=q[:], func=ACT.Abs_reciprocal_sqrt, bias=one_col)
+            inv_len = per_tile.tile([P, CAPS], F32)
+            nc.scalar.activation(out=inv_len[:], in_=q[:], func=ACT.Abs_reciprocal_sqrt, bias=eps_col)
             inv_one_plus_q = per_tile.tile([P, CAPS], F32)
             nc.scalar.activation(out=inv_one_plus_q[:], in_=inv_root[:], func=ACT.Square)
             h = per_tile.tile([P, CAPS], F32)
@@ -114,7 +116,7 @@ def tile_capsulenetwork_pc_s_kernel(tc, s, Wc, bc, out):
             nc.gpsimd.tensor_tensor(out=one_plus_q_h[:], in0=qh[:], in1=h[:], op=ALU.add)
             qh_of[i], one_plus_q_h_of[i] = qh, one_plus_q_h
 
-        def newton_step(i):
+        def newton_residual(i):
             one_plus_q_h_sq = per_tile.tile([P, CAPS], F32)
             nc.scalar.activation(out=one_plus_q_h_sq[:], in_=one_plus_q_h_of[i][:], func=ACT.Square)
             x_h_h = per_tile.tile([P, CAPS], F32)
@@ -126,6 +128,10 @@ def tile_capsulenetwork_pc_s_kernel(tc, s, Wc, bc, out):
                 op0=ALU.add,
                 op1=ALU.mult,
             )
+            x_h_h_of[i] = x_h_h
+
+        def newton_step(i):
+            x_h_h = x_h_h_of[i]
             doubled = [P, CAPS, PARTS_PER_CAP]
             factor = per_tile.tile(doubled, F32)
             nc.vector.scalar_tensor_tensor(
@@ -169,12 +175,15 @@ def tile_capsulenetwork_pc_s_kernel(tc, s, Wc, bc, out):
                 in1=fT[:].unsqueeze(2).unsqueeze(3).to_broadcast(grouped),
                 op=ALU.mult,
             )
+            v_grouped_of[i] = v_grouped
+
+        def quantise_and_matmul(i):
             v_codes = per_tile.tile([P, PASSES * P], U32, align_bytes=64)
             v_scales = per_tile.tile([P, PASSES * P], U8, align_bytes=64)
             nc.vector.quantize_mx(
                 out=v_codes[:].bitcast(FP8X4),
                 scales=v_scales[:],
-                in_=v_grouped[:].rearrange("p n u e -> p (n u e)"),
+                in_=v_grouped_of[i][:].rearrange("p n u e -> p (n u e)"),
             )
             acc = psum_o.tile([P, N_OUT], F32)
             for g in range(PASSES):
@@ -203,6 +212,10 @@ def tile_capsulenetwork_pc_s_kernel(tc, s, Wc, bc, out):
                 sum_squares(step)
             if is_tile(step - LAG_GUESS):
                 first_guess(step - LAG_GUESS)
+            if is_tile(step - LAG_NEWTON):
+                newton_residual(step - LAG_NEWTON)
+            if is_tile(step - LAG_QUANTISE):
+                quantise_and_matmul(step - LAG_QUANTISE)
             if is_tile(step - LAG_NEWTON):
                 newton_step(step - LAG_NEWTON)
             if is_tile(step - LAG_MULTIPLY):

@@ -12,6 +12,7 @@ ACT = mybir.ActivationFunctionType
 ALU = mybir.AluOpType
 
 P = 128
+MX_ALIGN = 64
 PACK = 4
 K_PASS = P * PACK
 
@@ -21,7 +22,6 @@ CAP_LEN = 8
 K_TOTAL = CAPS * CAP_LEN
 N_OUT = 128
 SQ_EPS = 1e-8
-NEWTON_SCALE = -0.5
 
 B_TILES = BATCH // P
 PASSES = K_TOTAL // K_PASS
@@ -30,12 +30,18 @@ PARTS_PER_CAP = CAP_LEN // PACK
 WORD = 2
 WORDS_PER_PART = PACK // WORD
 
+NEWTON_SHIFT = 3.0
+NEWTON_SCALE = -0.5
+
 LAG_GUESS = 2
-LAG_NEWTON = 3
-LAG_MULTIPLY = 4
-LAG_QUANTISE = 5
-LAG_STORE = 6
+LAG_NEWTON = LAG_GUESS + 1
+LAG_MULTIPLY = LAG_NEWTON + 1
+LAG_QUANTISE = LAG_MULTIPLY + 1
+LAG_STORE = LAG_QUANTISE + 1
+
 S_BANKS = LAG_MULTIPLY
+F_BANKS = 2
+OUT_BANKS = 2
 
 FLOPS = 2 * BATCH * K_TOTAL * N_OUT
 
@@ -50,8 +56,8 @@ def tile_capsulenetwork_pc_s_kernel(tc, s, Wc, bc, out):
         keep = ctx.enter_context(tc.tile_pool(name="keep", bufs=1))
         per_tile = ctx.enter_context(tc.tile_pool(name="per_tile", bufs=B_TILES))
         psum_s = ctx.enter_context(tc.psum_pool(name="psum_s", bufs=S_BANKS))
-        psum_f = ctx.enter_context(tc.psum_pool(name="psum_f", bufs=2))
-        psum_o = ctx.enter_context(tc.psum_pool(name="psum_o", bufs=2))
+        psum_f = ctx.enter_context(tc.psum_pool(name="psum_f", bufs=F_BANKS))
+        psum_o = ctx.enter_context(tc.psum_pool(name="psum_o", bufs=OUT_BANKS))
 
         const_cols = keep.tile([P, 2], F32)
         nc.vector.memset(const_cols[:, 0:1], SQ_EPS)
@@ -75,10 +81,10 @@ def tile_capsulenetwork_pc_s_kernel(tc, s, Wc, bc, out):
             nc.sync.dma_start(out=s_tiles[i][:], in_=s_rows[i])
         nc.sync.dma_start(out=bias[:], in_=bc.partition_broadcast(P))
 
-        w_grouped = keep.tile([P, PASSES, N_OUT, PACK], BF16, align_bytes=64)
+        w_grouped = keep.tile([P, PASSES, N_OUT, PACK], BF16, align_bytes=MX_ALIGN)
         nc.vector.tensor_copy(out=w_grouped[:], in_=w_raw[:].rearrange("p g t n -> p g n t"))
-        w_codes = keep.tile([P, PASSES, N_OUT], U32, align_bytes=64)
-        w_scales = keep.tile([P, PASSES, N_OUT], U8, align_bytes=64)
+        w_codes = keep.tile([P, PASSES, N_OUT], U32, align_bytes=MX_ALIGN)
+        w_scales = keep.tile([P, PASSES, N_OUT], U8, align_bytes=MX_ALIGN)
         nc.vector.quantize_mx(
             out=w_codes[:].rearrange("p g n -> p (g n)").bitcast(FP8X4),
             scales=w_scales[:].rearrange("p g n -> p (g n)"),
@@ -108,12 +114,18 @@ def tile_capsulenetwork_pc_s_kernel(tc, s, Wc, bc, out):
             nc.scalar.activation(out=inv_len[:], in_=q[:], func=ACT.Abs_reciprocal_sqrt, bias=eps_col)
             inv_one_plus_q = per_tile.tile([P, CAPS], F32)
             nc.scalar.activation(out=inv_one_plus_q[:], in_=inv_root[:], func=ACT.Square)
-            h = per_tile.tile([P, CAPS], F32)
-            nc.gpsimd.tensor_tensor(out=h[:], in0=inv_len[:], in1=inv_one_plus_q[:], op=ALU.mult)
+            q_inv_len = per_tile.tile([P, CAPS], F32)
+            nc.gpsimd.tensor_tensor(out=q_inv_len[:], in0=q[:], in1=inv_len[:], op=ALU.mult)
+            one_plus_q_inv_len = per_tile.tile([P, CAPS], F32)
+            nc.gpsimd.tensor_tensor(
+                out=one_plus_q_inv_len[:], in0=q_inv_len[:], in1=inv_len[:], op=ALU.add
+            )
             qh = per_tile.tile([P, CAPS], F32)
-            nc.gpsimd.tensor_tensor(out=qh[:], in0=q[:], in1=h[:], op=ALU.mult)
+            nc.gpsimd.tensor_tensor(out=qh[:], in0=q_inv_len[:], in1=inv_one_plus_q[:], op=ALU.mult)
             one_plus_q_h = per_tile.tile([P, CAPS], F32)
-            nc.gpsimd.tensor_tensor(out=one_plus_q_h[:], in0=qh[:], in1=h[:], op=ALU.add)
+            nc.gpsimd.tensor_tensor(
+                out=one_plus_q_h[:], in0=one_plus_q_inv_len[:], in1=inv_one_plus_q[:], op=ALU.mult
+            )
             qh_of[i], one_plus_q_h_of[i] = qh, one_plus_q_h
 
         def newton_residual(i):
@@ -137,7 +149,7 @@ def tile_capsulenetwork_pc_s_kernel(tc, s, Wc, bc, out):
             nc.vector.scalar_tensor_tensor(
                 out=factor[:],
                 in0=x_h_h[:].unsqueeze(2).to_broadcast(doubled),
-                scalar=-3.0,
+                scalar=-NEWTON_SHIFT,
                 in1=qh_of[i][:].unsqueeze(2).to_broadcast(doubled),
                 op0=ALU.add,
                 op1=ALU.mult,
@@ -166,7 +178,7 @@ def tile_capsulenetwork_pc_s_kernel(tc, s, Wc, bc, out):
                 out=fT[:], in_=fT_psum_of[i][:].rearrange("p g b -> p (g b)"), mul=NEWTON_SCALE
             )
             grouped = [P, PASSES * P, WORDS_PER_PART, WORD]
-            v_grouped = per_tile.tile(grouped, BF16, align_bytes=64)
+            v_grouped = per_tile.tile(grouped, BF16, align_bytes=MX_ALIGN)
             nc.vector.tensor_tensor(
                 out=v_grouped[:],
                 in0=sT_of[i][:].rearrange("p u g b -> p u (g b)").bitcast(BF16).rearrange(
@@ -178,8 +190,8 @@ def tile_capsulenetwork_pc_s_kernel(tc, s, Wc, bc, out):
             v_grouped_of[i] = v_grouped
 
         def quantise_and_matmul(i):
-            v_codes = per_tile.tile([P, PASSES * P], U32, align_bytes=64)
-            v_scales = per_tile.tile([P, PASSES * P], U8, align_bytes=64)
+            v_codes = per_tile.tile([P, PASSES * P], U32, align_bytes=MX_ALIGN)
+            v_scales = per_tile.tile([P, PASSES * P], U8, align_bytes=MX_ALIGN)
             nc.vector.quantize_mx(
                 out=v_codes[:].bitcast(FP8X4),
                 scales=v_scales[:],

@@ -33,15 +33,20 @@ WORDS_PER_PART = PACK // WORD
 NEWTON_SHIFT = 3.0
 NEWTON_SCALE = -0.5
 
+H_SCALE = 2.0**96
+H_SCALE_ROOT = 2.0**48
+
 LAG_GUESS = 2
-LAG_NEWTON = LAG_GUESS + 1
+LAG_PRODUCTS = LAG_GUESS + 1
+LAG_NEWTON = LAG_PRODUCTS + 1
 LAG_MULTIPLY = LAG_NEWTON + 1
 LAG_QUANTISE = LAG_MULTIPLY + 1
 LAG_STORE = LAG_QUANTISE + 1
 
-S_BANKS = LAG_MULTIPLY
+S_BANKS = 4
 F_BANKS = 2
 OUT_BANKS = 2
+LAG_TRANSPOSE = LAG_MULTIPLY - S_BANKS
 
 FLOPS = 2 * BATCH * K_TOTAL * N_OUT
 
@@ -91,7 +96,7 @@ def tile_capsulenetwork_pc_s_kernel(tc, s, Wc, bc, out):
             in_=w_grouped[:].rearrange("p g n t -> p (g n t)"),
         )
 
-        q_of, qh_of, one_plus_q_h_of, x_h_h_of = {}, {}, {}, {}
+        q_of, h_of, qh_of, one_plus_q_h_of, x_h_h_of = {}, {}, {}, {}, {}
         fT_psum_of, sT_of, v_grouped_of, acc_of = {}, {}, {}, {}
 
         def sum_squares(i):
@@ -113,24 +118,28 @@ def tile_capsulenetwork_pc_s_kernel(tc, s, Wc, bc, out):
             inv_len = per_tile.tile([P, CAPS], F32)
             nc.scalar.activation(out=inv_len[:], in_=q[:], func=ACT.Abs_reciprocal_sqrt, bias=eps_col)
             inv_one_plus_q = per_tile.tile([P, CAPS], F32)
-            nc.scalar.activation(out=inv_one_plus_q[:], in_=inv_root[:], func=ACT.Square)
-            q_inv_len = per_tile.tile([P, CAPS], F32)
-            nc.gpsimd.tensor_tensor(out=q_inv_len[:], in0=q[:], in1=inv_len[:], op=ALU.mult)
-            one_plus_q_inv_len = per_tile.tile([P, CAPS], F32)
-            nc.gpsimd.tensor_tensor(
-                out=one_plus_q_inv_len[:], in0=q_inv_len[:], in1=inv_len[:], op=ALU.add
+            nc.scalar.activation(
+                out=inv_one_plus_q[:], in_=inv_root[:], func=ACT.Square, scale=H_SCALE_ROOT
             )
+            h = per_tile.tile([P, CAPS], F32)
+            nc.gpsimd.tensor_tensor(out=h[:], in0=inv_len[:], in1=inv_one_plus_q[:], op=ALU.mult)
+            h_of[i] = h
+
+        def guess_times_q(i):
             qh = per_tile.tile([P, CAPS], F32)
-            nc.gpsimd.tensor_tensor(out=qh[:], in0=q_inv_len[:], in1=inv_one_plus_q[:], op=ALU.mult)
+            nc.gpsimd.tensor_tensor(out=qh[:], in0=q_of[i][:], in1=h_of[i][:], op=ALU.mult)
+            qh_of[i] = qh
+
+        def guess_times_one_plus_q(i):
             one_plus_q_h = per_tile.tile([P, CAPS], F32)
-            nc.gpsimd.tensor_tensor(
-                out=one_plus_q_h[:], in0=one_plus_q_inv_len[:], in1=inv_one_plus_q[:], op=ALU.mult
-            )
-            qh_of[i], one_plus_q_h_of[i] = qh, one_plus_q_h
+            nc.gpsimd.tensor_tensor(out=one_plus_q_h[:], in0=qh_of[i][:], in1=h_of[i][:], op=ALU.add)
+            one_plus_q_h_of[i] = one_plus_q_h
 
         def newton_residual(i):
             one_plus_q_h_sq = per_tile.tile([P, CAPS], F32)
-            nc.scalar.activation(out=one_plus_q_h_sq[:], in_=one_plus_q_h_of[i][:], func=ACT.Square)
+            nc.scalar.activation(
+                out=one_plus_q_h_sq[:], in_=one_plus_q_h_of[i][:], func=ACT.Square, scale=1.0 / H_SCALE
+            )
             x_h_h = per_tile.tile([P, CAPS], F32)
             nc.vector.scalar_tensor_tensor(
                 out=x_h_h[:],
@@ -175,7 +184,9 @@ def tile_capsulenetwork_pc_s_kernel(tc, s, Wc, bc, out):
         def multiply(i):
             fT = per_tile.tile([P, PASSES * P], F32)
             nc.scalar.mul(
-                out=fT[:], in_=fT_psum_of[i][:].rearrange("p g b -> p (g b)"), mul=NEWTON_SCALE
+                out=fT[:],
+                in_=fT_psum_of[i][:].rearrange("p g b -> p (g b)"),
+                mul=NEWTON_SCALE / H_SCALE,
             )
             grouped = [P, PASSES * P, WORDS_PER_PART, WORD]
             v_grouped = per_tile.tile(grouped, BF16, align_bytes=MX_ALIGN)
@@ -222,8 +233,12 @@ def tile_capsulenetwork_pc_s_kernel(tc, s, Wc, bc, out):
         for step in range(B_TILES + LAG_STORE):
             if is_tile(step):
                 sum_squares(step)
+            if is_tile(step - LAG_PRODUCTS):
+                guess_times_q(step - LAG_PRODUCTS)
             if is_tile(step - LAG_GUESS):
                 first_guess(step - LAG_GUESS)
+            if is_tile(step - LAG_PRODUCTS):
+                guess_times_one_plus_q(step - LAG_PRODUCTS)
             if is_tile(step - LAG_NEWTON):
                 newton_residual(step - LAG_NEWTON)
             if is_tile(step - LAG_QUANTISE):
@@ -232,7 +247,7 @@ def tile_capsulenetwork_pc_s_kernel(tc, s, Wc, bc, out):
                 newton_step(step - LAG_NEWTON)
             if is_tile(step - LAG_MULTIPLY):
                 multiply(step - LAG_MULTIPLY)
-            if is_tile(step):
-                transpose_s(step)
+            if is_tile(step - LAG_TRANSPOSE):
+                transpose_s(step - LAG_TRANSPOSE)
             if is_tile(step - LAG_STORE):
                 add_bias_and_store(step - LAG_STORE)

@@ -14,7 +14,6 @@ ALU = mybir.AluOpType
 P = 128
 MX_ALIGN = 64
 PACK = 4
-K_PASS = P * PACK
 
 BATCH = 768
 CAPS = 128
@@ -24,29 +23,24 @@ N_OUT = 128
 SQ_EPS = 1e-8
 
 B_TILES = BATCH // P
-PASSES = K_TOTAL // K_PASS
-CAPS_PER_PASS = CAPS // PASSES
-PARTS_PER_CAP = CAP_LEN // PACK
+PASSES = CAP_LEN // PACK
 WORD = 2
-WORDS_PER_PART = PACK // WORD
+CAP_WORDS = CAP_LEN // WORD
+WORDS_PER_PASS = PACK // WORD
+
+N_A, N_HALF, N_Z = 4, 2, 16
 
 NEWTON_SHIFT = 3.0
 NEWTON_SCALE = -0.5
-
 H_SCALE = 2.0**96
 H_SCALE_ROOT = 2.0**48
 
-LAG_GUESS = 2
-LAG_PRODUCTS = LAG_GUESS + 1
-LAG_NEWTON = LAG_PRODUCTS + 1
-LAG_MULTIPLY = LAG_NEWTON + 1
-LAG_QUANTISE = LAG_MULTIPLY + 1
-LAG_STORE = LAG_QUANTISE + 1
-
 S_BANKS = 4
-F_BANKS = 2
+Q_BANKS = 2
 OUT_BANKS = 2
-LAG_TRANSPOSE = LAG_MULTIPLY - S_BANKS
+
+EARLY_LOADS = 3
+HEAD_TILES = 1
 
 FLOPS = 2 * BATCH * K_TOTAL * N_OUT
 
@@ -61,7 +55,7 @@ def tile_capsulenetwork_pc_s_kernel(tc, s, Wc, bc, out):
         keep = ctx.enter_context(tc.tile_pool(name="keep", bufs=1))
         per_tile = ctx.enter_context(tc.tile_pool(name="per_tile", bufs=B_TILES))
         psum_s = ctx.enter_context(tc.psum_pool(name="psum_s", bufs=S_BANKS))
-        psum_f = ctx.enter_context(tc.psum_pool(name="psum_f", bufs=F_BANKS))
+        psum_q = ctx.enter_context(tc.psum_pool(name="psum_q", bufs=Q_BANKS))
         psum_o = ctx.enter_context(tc.psum_pool(name="psum_o", bufs=OUT_BANKS))
 
         const_cols = keep.tile([P, 2], F32)
@@ -78,127 +72,135 @@ def tile_capsulenetwork_pc_s_kernel(tc, s, Wc, bc, out):
         for i in range(B_TILES):
             s_tile = per_tile.tile([P, K_TOTAL], BF16)
             s_tiles.append(s_tile)
-        w_raw = keep.tile([P, PASSES, PACK, N_OUT], BF16)
+        w_raw = keep.tile([P, CAP_LEN, N_OUT], BF16)
         bias = keep.tile([P, N_OUT], BF16)
-        nc.sync.dma_start(out=s_tiles[0][:], in_=s_rows[0])
-        nc.sync.dma_start(out=w_raw[:], in_=Wc.rearrange("(g p t) n -> p g t n", g=PASSES, t=PACK))
-        for i in range(1, B_TILES):
+        w_caps = Wc.rearrange("(c z o) n -> c z (o n)", z=N_Z, o=CAP_LEN)
+        for i in range(EARLY_LOADS):
+            nc.sync.dma_start(out=s_tiles[i][:], in_=s_rows[i])
+        for c in range(N_A * N_HALF):
+            first = (c // N_HALF) * (N_HALF * N_Z) + c % N_HALF
+            nc.sync.dma_start(
+                out=w_raw[first : first + N_HALF * (N_Z - 1) + 1 : N_HALF, :, :].rearrange("p o n -> p (o n)"),
+                in_=w_caps[c],
+            )
+        for i in range(EARLY_LOADS, B_TILES):
             nc.sync.dma_start(out=s_tiles[i][:], in_=s_rows[i])
         nc.sync.dma_start(out=bias[:], in_=bc.partition_broadcast(P))
 
-        w_grouped = keep.tile([P, PASSES, N_OUT, PACK], BF16, align_bytes=MX_ALIGN)
-        nc.vector.tensor_copy(out=w_grouped[:], in_=w_raw[:].rearrange("p g t n -> p g n t"))
         w_codes = keep.tile([P, PASSES, N_OUT], U32, align_bytes=MX_ALIGN)
         w_scales = keep.tile([P, PASSES, N_OUT], U8, align_bytes=MX_ALIGN)
-        nc.vector.quantize_mx(
-            out=w_codes[:].rearrange("p g n -> p (g n)").bitcast(FP8X4),
-            scales=w_scales[:].rearrange("p g n -> p (g n)"),
-            in_=w_grouped[:].rearrange("p g n t -> p (g n t)"),
-        )
 
-        q_of, h_of, qh_of, one_plus_q_h_of, x_h_h_of = {}, {}, {}, {}, {}
-        fT_psum_of, sT_of, v_grouped_of, acc_of = {}, {}, {}, {}
+        def quantise_weights():
+            w_grouped = keep.tile([P, PASSES, N_OUT, PACK], BF16, align_bytes=MX_ALIGN)
+            nc.vector.tensor_copy(
+                out=w_grouped[:], in_=w_raw[:].rearrange("p (g t) n -> p g n t", t=PACK)
+            )
+            nc.vector.quantize_mx(
+                out=w_codes[:].rearrange("p g n -> p (g n)").bitcast(FP8X4),
+                scales=w_scales[:].rearrange("p g n -> p (g n)"),
+                in_=w_grouped[:].rearrange("p g n t -> p (g n t)"),
+            )
+
+        words_of, squares_of, qT_of, q_of, inv_len_of, inv_1q_of = {}, {}, {}, {}, {}, {}
+        h_of, qh_of, ph_of, ph_sq_of, x_of, f_of = {}, {}, {}, {}, {}, {}
+        sT_of, v_of, acc_of, qh_true_of = {}, {}, {}, {}
+
+        def order_words(i):
+            words = per_tile.tile([P, CAPS, CAP_WORDS], F32)
+            nc.vector.tensor_copy(
+                out=words[:].rearrange("b (A z a) w -> b A z a w", A=N_A, z=N_Z),
+                in_=s_tiles[i][:].bitcast(F32).rearrange(
+                    "b (A a z w) -> b A z a w", A=N_A, a=N_HALF, z=N_Z
+                ),
+            )
+            words_of[i] = words
+
+        def square(i):
+            squares = per_tile.tile([P, CAPS, CAP_LEN], F32)
+            nc.scalar.activation(
+                out=squares[:].rearrange("b c o -> b (c o)"),
+                in_=words_of[i][:].rearrange("b c w -> b (c w)").bitcast(BF16),
+                func=ACT.Square,
+            )
+            squares_of[i] = squares
 
         def sum_squares(i):
-            squares = per_tile.tile([P, K_TOTAL], F32)
-            nc.scalar.activation(out=squares[:], in_=s_tiles[i][:], func=ACT.Square)
-            q = per_tile.tile([P, CAPS], F32)
-            nc.vector.tensor_reduce(
-                out=q[:],
-                in_=squares[:].rearrange("b (j o) -> b j o", o=CAP_LEN),
-                axis=mybir.AxisListType.X,
-                op=ALU.add,
-            )
-            q_of[i] = q
-
-        def first_guess(i):
-            q = q_of[i]
-            inv_root = per_tile.tile([P, CAPS], F32)
-            nc.scalar.activation(out=inv_root[:], in_=q[:], func=ACT.Abs_reciprocal_sqrt, bias=one_col)
-            inv_len = per_tile.tile([P, CAPS], F32)
-            nc.scalar.activation(out=inv_len[:], in_=q[:], func=ACT.Abs_reciprocal_sqrt, bias=eps_col)
-            inv_one_plus_q = per_tile.tile([P, CAPS], F32)
-            nc.scalar.activation(
-                out=inv_one_plus_q[:], in_=inv_root[:], func=ACT.Square, scale=H_SCALE_ROOT
-            )
-            h = per_tile.tile([P, CAPS], F32)
-            nc.gpsimd.tensor_tensor(out=h[:], in0=inv_len[:], in1=inv_one_plus_q[:], op=ALU.mult)
-            h_of[i] = h
-
-        def guess_times_q(i):
-            qh = per_tile.tile([P, CAPS], F32)
-            nc.gpsimd.tensor_tensor(out=qh[:], in0=q_of[i][:], in1=h_of[i][:], op=ALU.mult)
-            qh_of[i] = qh
-
-        def guess_times_one_plus_q(i):
-            one_plus_q_h = per_tile.tile([P, CAPS], F32)
-            nc.gpsimd.tensor_tensor(out=one_plus_q_h[:], in0=qh_of[i][:], in1=h_of[i][:], op=ALU.add)
-            one_plus_q_h_of[i] = one_plus_q_h
-
-        def newton_residual(i):
-            one_plus_q_h_sq = per_tile.tile([P, CAPS], F32)
-            nc.scalar.activation(
-                out=one_plus_q_h_sq[:], in_=one_plus_q_h_of[i][:], func=ACT.Square, scale=1.0 / H_SCALE
-            )
-            x_h_h = per_tile.tile([P, CAPS], F32)
-            nc.vector.scalar_tensor_tensor(
-                out=x_h_h[:],
-                in0=q_of[i][:],
-                scalar=SQ_EPS,
-                in1=one_plus_q_h_sq[:],
-                op0=ALU.add,
-                op1=ALU.mult,
-            )
-            x_h_h_of[i] = x_h_h
-
-        def newton_step(i):
-            x_h_h = x_h_h_of[i]
-            doubled = [P, CAPS, PARTS_PER_CAP]
-            factor = per_tile.tile(doubled, F32)
-            nc.vector.scalar_tensor_tensor(
-                out=factor[:],
-                in0=x_h_h[:].unsqueeze(2).to_broadcast(doubled),
-                scalar=-NEWTON_SHIFT,
-                in1=qh_of[i][:].unsqueeze(2).to_broadcast(doubled),
-                op0=ALU.add,
-                op1=ALU.mult,
-            )
-            fT_psum = psum_f.tile([P, PASSES, P], F32)
-            for g in range(PASSES):
-                caps = slice(g * CAPS_PER_PASS, (g + 1) * CAPS_PER_PASS)
-                nc.tensor.transpose(
-                    fT_psum[:, g, :], factor[:, caps, :].rearrange("b j d -> b (j d)"), ident[:]
+            qT = psum_q.tile([P, P], F32)
+            for o in range(CAP_LEN):
+                nc.tensor.matmul(
+                    out=qT[:],
+                    lhsT=squares_of[i][:, :, o],
+                    rhs=ident[:],
+                    is_transpose=True,
+                    start=(o == 0),
+                    stop=(o == CAP_LEN - 1),
                 )
-            fT_psum_of[i] = fT_psum
+            qT_of[i] = qT
 
         def transpose_s(i):
-            s_words = s_tiles[i][:].bitcast(F32).rearrange(
-                "b (g p u) -> b g u p", g=PASSES, u=WORDS_PER_PART
-            )
-            sT = psum_s.tile([P, WORDS_PER_PART, PASSES, P], F32)
+            sT = psum_s.tile([P, WORDS_PER_PASS, PASSES, P], F32)
             for g in range(PASSES):
-                for u in range(WORDS_PER_PART):
-                    nc.tensor.transpose(sT[:, u, g, :], s_words[:, g, u, :], ident[:])
+                for u in range(WORDS_PER_PASS):
+                    nc.tensor.transpose(
+                        sT[:, u, g, :], words_of[i][:, :, g * WORDS_PER_PASS + u], ident[:]
+                    )
             sT_of[i] = sT
 
+        def guesses(i):
+            qT = qT_of[i]
+            inv_root = per_tile.tile([P, P], F32)
+            nc.scalar.activation(out=inv_root[:], in_=qT[:], func=ACT.Abs_reciprocal_sqrt, bias=one_col)
+            inv_len = per_tile.tile([P, P], F32)
+            nc.scalar.activation(out=inv_len[:], in_=qT[:], func=ACT.Abs_reciprocal_sqrt, bias=eps_col)
+            inv_1q = per_tile.tile([P, P], F32)
+            nc.scalar.activation(out=inv_1q[:], in_=inv_root[:], func=ACT.Square, scale=H_SCALE_ROOT)
+            q = per_tile.tile([P, P], F32)
+            nc.scalar.copy(out=q[:], in_=qT[:])
+            inv_len_of[i], inv_1q_of[i], q_of[i] = inv_len, inv_1q, q
+
+        def products(i):
+            eng = nc.vector if i < HEAD_TILES else nc.gpsimd
+            h = per_tile.tile([P, P], F32)
+            eng.tensor_tensor(out=h[:], in0=inv_len_of[i][:], in1=inv_1q_of[i][:], op=ALU.mult)
+            qh = per_tile.tile([P, P], F32)
+            eng.tensor_tensor(out=qh[:], in0=q_of[i][:], in1=h[:], op=ALU.mult)
+            ph = per_tile.tile([P, P], F32)
+            eng.tensor_tensor(out=ph[:], in0=qh[:], in1=h[:], op=ALU.add)
+            h_of[i], qh_of[i], ph_of[i] = h, qh, ph
+
+        def residual_square(i):
+            ph_sq = per_tile.tile([P, P], F32)
+            nc.scalar.activation(out=ph_sq[:], in_=ph_of[i][:], func=ACT.Square, scale=1.0 / H_SCALE)
+            ph_sq_of[i] = ph_sq
+            qh_true = per_tile.tile([P, P], F32)
+            nc.scalar.mul(out=qh_true[:], in_=qh_of[i][:], mul=NEWTON_SCALE / H_SCALE)
+            qh_true_of[i] = qh_true
+
+        def residual(i):
+            x = per_tile.tile([P, P], F32)
+            nc.vector.scalar_tensor_tensor(
+                out=x[:], in0=q_of[i][:], scalar=SQ_EPS, in1=ph_sq_of[i][:], op0=ALU.add, op1=ALU.mult
+            )
+            x_of[i] = x
+
+        def newton(i):
+            f = per_tile.tile([P, P], F32)
+            nc.vector.scalar_tensor_tensor(
+                out=f[:], in0=x_of[i][:], scalar=-NEWTON_SHIFT, in1=qh_true_of[i][:], op0=ALU.add, op1=ALU.mult
+            )
+            f_of[i] = f
+
         def multiply(i):
-            fT = per_tile.tile([P, PASSES * P], F32)
-            nc.scalar.mul(
-                out=fT[:],
-                in_=fT_psum_of[i][:].rearrange("p g b -> p (g b)"),
-                mul=NEWTON_SCALE / H_SCALE,
-            )
-            grouped = [P, PASSES * P, WORDS_PER_PART, WORD]
-            v_grouped = per_tile.tile(grouped, BF16, align_bytes=MX_ALIGN)
-            nc.vector.tensor_tensor(
-                out=v_grouped[:],
-                in0=sT_of[i][:].rearrange("p u g b -> p u (g b)").bitcast(BF16).rearrange(
-                    "p u (n e) -> p n u e", e=WORD
-                ),
-                in1=fT[:].unsqueeze(2).unsqueeze(3).to_broadcast(grouped),
-                op=ALU.mult,
-            )
-            v_grouped_of[i] = v_grouped
+            shape = [P, P, WORDS_PER_PASS, WORD]
+            v = per_tile.tile([P, PASSES, P, PACK], BF16, align_bytes=MX_ALIGN)
+            for g in range(PASSES):
+                nc.vector.tensor_tensor(
+                    out=v[:, g, :, :].rearrange("p b (u e) -> p b u e", e=WORD),
+                    in0=sT_of[i][:, :, g, :].bitcast(BF16).rearrange("p u (b e) -> p b u e", e=WORD),
+                    in1=f_of[i][:].unsqueeze(2).unsqueeze(3).to_broadcast(shape),
+                    op=ALU.mult,
+                )
+            v_of[i] = v
 
         def quantise_and_matmul(i):
             v_codes = per_tile.tile([P, PASSES * P], U32, align_bytes=MX_ALIGN)
@@ -206,7 +208,7 @@ def tile_capsulenetwork_pc_s_kernel(tc, s, Wc, bc, out):
             nc.vector.quantize_mx(
                 out=v_codes[:].bitcast(FP8X4),
                 scales=v_scales[:],
-                in_=v_grouped_of[i][:].rearrange("p n u e -> p (n u e)"),
+                in_=v_of[i][:].rearrange("p g b t -> p (g b t)"),
             )
             acc = psum_o.tile([P, N_OUT], F32)
             for g in range(PASSES):
@@ -230,24 +232,32 @@ def tile_capsulenetwork_pc_s_kernel(tc, s, Wc, bc, out):
         def is_tile(i):
             return 0 <= i < B_TILES
 
-        for step in range(B_TILES + LAG_STORE):
+        for i in range(EARLY_LOADS):
+            order_words(i)
+        quantise_weights()
+
+        for step in range(B_TILES + 5):
             if is_tile(step):
+                square(step)
                 sum_squares(step)
-            if is_tile(step - LAG_PRODUCTS):
-                guess_times_q(step - LAG_PRODUCTS)
-            if is_tile(step - LAG_GUESS):
-                first_guess(step - LAG_GUESS)
-            if is_tile(step - LAG_PRODUCTS):
-                guess_times_one_plus_q(step - LAG_PRODUCTS)
-            if is_tile(step - LAG_NEWTON):
-                newton_residual(step - LAG_NEWTON)
-            if is_tile(step - LAG_QUANTISE):
-                quantise_and_matmul(step - LAG_QUANTISE)
-            if is_tile(step - LAG_NEWTON):
-                newton_step(step - LAG_NEWTON)
-            if is_tile(step - LAG_MULTIPLY):
-                multiply(step - LAG_MULTIPLY)
-            if is_tile(step - LAG_TRANSPOSE):
-                transpose_s(step - LAG_TRANSPOSE)
-            if is_tile(step - LAG_STORE):
-                add_bias_and_store(step - LAG_STORE)
+            if is_tile(step - 2) and step - 2 < HEAD_TILES:
+                residual_square(step - 2)
+            if is_tile(step - 1):
+                guesses(step - 1)
+                products(step - 1)
+            if step >= 1 and is_tile(step - 1 + EARLY_LOADS):
+                order_words(step - 1 + EARLY_LOADS)
+            if is_tile(step - 2) and step - 2 >= HEAD_TILES:
+                residual_square(step - 2)
+            if is_tile(step - 2):
+                transpose_s(step - 2)
+            if is_tile(step - 3):
+                multiply(step - 3)
+            if is_tile(step - 2):
+                residual(step - 2)
+            if is_tile(step - 3):
+                quantise_and_matmul(step - 3)
+            if is_tile(step - 2):
+                newton(step - 2)
+            if is_tile(step - 4):
+                add_bias_and_store(step - 4)

@@ -35,11 +35,12 @@ NEWTON_SCALE = -0.5
 H_SCALE = 2.0**96
 H_SCALE_ROOT = 2.0**48
 
-S_BANKS = 4
-Q_BANKS = 2
+S_BANKS = 3
+Q_BANKS = 3
 OUT_BANKS = 2
 
-EARLY_LOADS = 3
+LEAD = 3
+SHARED_SQUARES = 3
 HEAD_TILES = 1
 
 FLOPS = 2 * BATCH * K_TOTAL * N_OUT
@@ -75,7 +76,7 @@ def tile_capsulenetwork_pc_s_kernel(tc, s, Wc, bc, out):
         w_raw = keep.tile([P, CAP_LEN, N_OUT], BF16)
         bias = keep.tile([P, N_OUT], BF16)
         w_caps = Wc.rearrange("(c z o) n -> c z (o n)", z=N_Z, o=CAP_LEN)
-        for i in range(EARLY_LOADS):
+        for i in range(LEAD):
             nc.sync.dma_start(out=s_tiles[i][:], in_=s_rows[i])
         for c in range(N_A * N_HALF):
             first = (c // N_HALF) * (N_HALF * N_Z) + c % N_HALF
@@ -83,18 +84,29 @@ def tile_capsulenetwork_pc_s_kernel(tc, s, Wc, bc, out):
                 out=w_raw[first : first + N_HALF * (N_Z - 1) + 1 : N_HALF, :, :].rearrange("p o n -> p (o n)"),
                 in_=w_caps[c],
             )
-        for i in range(EARLY_LOADS, B_TILES):
+        for i in range(LEAD, B_TILES):
             nc.sync.dma_start(out=s_tiles[i][:], in_=s_rows[i])
         nc.sync.dma_start(out=bias[:], in_=bc.partition_broadcast(P))
 
         w_codes = keep.tile([P, PASSES, N_OUT], U32, align_bytes=MX_ALIGN)
         w_scales = keep.tile([P, PASSES, N_OUT], U8, align_bytes=MX_ALIGN)
 
-        def quantise_weights():
+        w_grouped_of = {}
+
+        def group_weights():
             w_grouped = keep.tile([P, PASSES, N_OUT, PACK], BF16, align_bytes=MX_ALIGN)
-            nc.vector.tensor_copy(
-                out=w_grouped[:], in_=w_raw[:].rearrange("p (g t) n -> p g n t", t=PACK)
+            nc.gpsimd.tensor_scalar(
+                out=w_grouped[:],
+                in0=w_raw[:].rearrange("p (g t) n -> p g n t", t=PACK),
+                scalar1=1.0,
+                scalar2=0.0,
+                op0=ALU.mult,
+                op1=ALU.add,
             )
+            w_grouped_of[0] = w_grouped
+
+        def quantise_weights():
+            w_grouped = w_grouped_of[0]
             nc.vector.quantize_mx(
                 out=w_codes[:].rearrange("p g n -> p (g n)").bitcast(FP8X4),
                 scales=w_scales[:].rearrange("p g n -> p (g n)"),
@@ -117,11 +129,15 @@ def tile_capsulenetwork_pc_s_kernel(tc, s, Wc, bc, out):
 
         def square(i):
             squares = per_tile.tile([P, CAPS, CAP_LEN], F32)
-            nc.scalar.activation(
-                out=squares[:].rearrange("b c o -> b (c o)"),
-                in_=words_of[i][:].rearrange("b c w -> b (c w)").bitcast(BF16),
-                func=ACT.Square,
-            )
+            as_it_came = s_tiles[i][:].rearrange("b (A a z o) -> b a A z o", A=N_A, a=N_HALF, z=N_Z)
+            ordered = squares[:].rearrange("b (A z a) o -> b a A z o", A=N_A, z=N_Z)
+            nc.scalar.activation(out=ordered[:, 0], in_=as_it_came[:, 0], func=ACT.Square)
+            if i < SHARED_SQUARES:
+                nc.vector.tensor_tensor(
+                    out=ordered[:, 1], in0=as_it_came[:, 1], in1=as_it_came[:, 1], op=ALU.mult
+                )
+            else:
+                nc.scalar.activation(out=ordered[:, 1], in_=as_it_came[:, 1], func=ACT.Square)
             squares_of[i] = squares
 
         def sum_squares(i):
@@ -232,32 +248,39 @@ def tile_capsulenetwork_pc_s_kernel(tc, s, Wc, bc, out):
         def is_tile(i):
             return 0 <= i < B_TILES
 
-        for i in range(EARLY_LOADS):
+        for i in range(LEAD):
+            square(i)
+            sum_squares(i)
+        for i in range(LEAD):
             order_words(i)
-        quantise_weights()
+        for i in range(2):
+            transpose_s(i)
+        group_weights()
+        for i in range(2):
+            guesses(i)
+            products(i)
 
-        for step in range(B_TILES + 5):
+        for step in range(B_TILES + 2):
             if is_tile(step):
-                square(step)
-                sum_squares(step)
-            if is_tile(step - 2) and step - 2 < HEAD_TILES:
-                residual_square(step - 2)
+                residual_square(step)
             if is_tile(step - 1):
-                guesses(step - 1)
-                products(step - 1)
-            if step >= 1 and is_tile(step - 1 + EARLY_LOADS):
-                order_words(step - 1 + EARLY_LOADS)
-            if is_tile(step - 2) and step - 2 >= HEAD_TILES:
-                residual_square(step - 2)
+                multiply(step - 1)
+            if is_tile(step):
+                residual(step)
+            if step == 1:
+                quantise_weights()
+            if is_tile(step - 1):
+                quantise_and_matmul(step - 1)
+            if is_tile(step):
+                newton(step)
             if is_tile(step - 2):
-                transpose_s(step - 2)
-            if is_tile(step - 3):
-                multiply(step - 3)
-            if is_tile(step - 2):
-                residual(step - 2)
-            if is_tile(step - 3):
-                quantise_and_matmul(step - 3)
-            if is_tile(step - 2):
-                newton(step - 2)
-            if is_tile(step - 4):
-                add_bias_and_store(step - 4)
+                add_bias_and_store(step - 2)
+            if step >= 1 and is_tile(step + 1):
+                transpose_s(step + 1)
+            if is_tile(step + LEAD):
+                square(step + LEAD)
+                sum_squares(step + LEAD)
+                order_words(step + LEAD)
+            if is_tile(step + 2):
+                guesses(step + 2)
+                products(step + 2)

@@ -1,3 +1,4 @@
+import math
 from contextlib import ExitStack
 
 import concourse.mybir as mybir
@@ -28,20 +29,14 @@ WORD = 2
 CAP_WORDS = CAP_LEN // WORD
 WORDS_PER_PASS = PACK // WORD
 
-N_A, N_HALF, N_Z = 4, 2, 16
+N_A, N_HALF, N_Z = 2, 2, 32
 
-NEWTON_SHIFT = 3.0
-NEWTON_SCALE = -0.5
-H_SCALE = 2.0**96
-H_SCALE_ROOT = 2.0**48
+SHIFT = 48.0
 
-S_BANKS = 3
-Q_BANKS = 3
+GROUP = 3
+S_BANKS = 4
+Q_BANKS = 2
 OUT_BANKS = 2
-
-LEAD = 3
-SHARED_SQUARES = 3
-HEAD_TILES = 1
 
 FLOPS = 2 * BATCH * K_TOTAL * N_OUT
 
@@ -55,67 +50,53 @@ def tile_capsulenetwork_pc_s_kernel(tc, s, Wc, bc, out):
         ctx.enter_context(tc.manual_schedule())
         keep = ctx.enter_context(tc.tile_pool(name="keep", bufs=1))
         per_tile = ctx.enter_context(tc.tile_pool(name="per_tile", bufs=B_TILES))
+        per_group = ctx.enter_context(tc.tile_pool(name="per_group", bufs=B_TILES // GROUP))
         psum_s = ctx.enter_context(tc.psum_pool(name="psum_s", bufs=S_BANKS))
         psum_q = ctx.enter_context(tc.psum_pool(name="psum_q", bufs=Q_BANKS))
         psum_o = ctx.enter_context(tc.psum_pool(name="psum_o", bufs=OUT_BANKS))
 
-        const_cols = keep.tile([P, 2], F32)
+        const_cols = keep.tile([P, 3], F32)
         nc.vector.memset(const_cols[:, 0:1], SQ_EPS)
         nc.vector.memset(const_cols[:, 1:2], 1.0)
+        nc.vector.memset(const_cols[:, 2:3], SHIFT)
         eps_col = const_cols[:, 0:1]
         one_col = const_cols[:, 1:2]
+        shift_col = const_cols[:, 2:3]
         table_warm = keep.tile([P, 1], F32)
-        nc.scalar.activation(out=table_warm[:], in_=one_col, func=ACT.Abs_reciprocal_sqrt)
+        nc.scalar.activation(out=table_warm[:], in_=one_col, func=ACT.Ln)
         ident = keep.tile([P, P], F32)
         make_identity(nc, ident[:])
 
         s_tiles = []
         for i in range(B_TILES):
             s_tile = per_tile.tile([P, K_TOTAL], BF16)
+            nc.sync.dma_start(out=s_tile[:], in_=s_rows[i])
             s_tiles.append(s_tile)
         w_raw = keep.tile([P, CAP_LEN, N_OUT], BF16)
-        bias = keep.tile([P, N_OUT], BF16)
         w_caps = Wc.rearrange("(c z o) n -> c z (o n)", z=N_Z, o=CAP_LEN)
-        for i in range(LEAD):
-            nc.sync.dma_start(out=s_tiles[i][:], in_=s_rows[i])
         for c in range(N_A * N_HALF):
             first = (c // N_HALF) * (N_HALF * N_Z) + c % N_HALF
             nc.sync.dma_start(
                 out=w_raw[first : first + N_HALF * (N_Z - 1) + 1 : N_HALF, :, :].rearrange("p o n -> p (o n)"),
                 in_=w_caps[c],
             )
-        for i in range(LEAD, B_TILES):
-            nc.sync.dma_start(out=s_tiles[i][:], in_=s_rows[i])
+        bias = keep.tile([P, N_OUT], BF16)
         nc.sync.dma_start(out=bias[:], in_=bc.partition_broadcast(P))
 
         w_codes = keep.tile([P, PASSES, N_OUT], U32, align_bytes=MX_ALIGN)
         w_scales = keep.tile([P, PASSES, N_OUT], U8, align_bytes=MX_ALIGN)
+        w_grouped = keep.tile([P, PASSES, N_OUT, PACK], BF16, align_bytes=MX_ALIGN)
+        nc.gpsimd.tensor_scalar(
+            out=w_grouped[:],
+            in0=w_raw[:].rearrange("p (g t) n -> p g n t", t=PACK),
+            scalar1=1.0,
+            scalar2=0.0,
+            op0=ALU.mult,
+            op1=ALU.add,
+        )
 
-        w_grouped_of = {}
-
-        def group_weights():
-            w_grouped = keep.tile([P, PASSES, N_OUT, PACK], BF16, align_bytes=MX_ALIGN)
-            nc.gpsimd.tensor_scalar(
-                out=w_grouped[:],
-                in0=w_raw[:].rearrange("p (g t) n -> p g n t", t=PACK),
-                scalar1=1.0,
-                scalar2=0.0,
-                op0=ALU.mult,
-                op1=ALU.add,
-            )
-            w_grouped_of[0] = w_grouped
-
-        def quantise_weights():
-            w_grouped = w_grouped_of[0]
-            nc.vector.quantize_mx(
-                out=w_codes[:].rearrange("p g n -> p (g n)").bitcast(FP8X4),
-                scales=w_scales[:].rearrange("p g n -> p (g n)"),
-                in_=w_grouped[:].rearrange("p g n t -> p (g n t)"),
-            )
-
-        words_of, squares_of, qT_of, q_of, inv_len_of, inv_1q_of = {}, {}, {}, {}, {}, {}
-        h_of, qh_of, ph_of, ph_sq_of, x_of, f_of = {}, {}, {}, {}, {}, {}
-        sT_of, v_of, acc_of, qh_true_of = {}, {}, {}, {}
+        words_of, squares_of, q_of, m_of, e_of, f_of = {}, {}, {}, {}, {}, {}
+        sT_of, v_of, acc_of = {}, {}, {}
 
         def order_words(i):
             words = per_tile.tile([P, CAPS, CAP_WORDS], F32)
@@ -132,26 +113,25 @@ def tile_capsulenetwork_pc_s_kernel(tc, s, Wc, bc, out):
             as_it_came = s_tiles[i][:].rearrange("b (A a z o) -> b a A z o", A=N_A, a=N_HALF, z=N_Z)
             ordered = squares[:].rearrange("b (A z a) o -> b a A z o", A=N_A, z=N_Z)
             nc.scalar.activation(out=ordered[:, 0], in_=as_it_came[:, 0], func=ACT.Square)
-            if i < SHARED_SQUARES:
-                nc.vector.tensor_tensor(
-                    out=ordered[:, 1], in0=as_it_came[:, 1], in1=as_it_came[:, 1], op=ALU.mult
-                )
-            else:
-                nc.scalar.activation(out=ordered[:, 1], in_=as_it_came[:, 1], func=ACT.Square)
+            nc.vector.tensor_tensor(
+                out=ordered[:, 1], in0=as_it_came[:, 1], in1=as_it_came[:, 1], op=ALU.mult
+            )
             squares_of[i] = squares
 
         def sum_squares(i):
-            qT = psum_q.tile([P, P], F32)
+            grp, slot = divmod(i, GROUP)
+            if slot == 0:
+                q_bank = psum_q.tile([P, GROUP, P], F32)
+                q_of[grp] = q_bank
             for o in range(CAP_LEN):
                 nc.tensor.matmul(
-                    out=qT[:],
+                    out=q_of[grp][:, slot, :],
                     lhsT=squares_of[i][:, :, o],
                     rhs=ident[:],
                     is_transpose=True,
                     start=(o == 0),
                     stop=(o == CAP_LEN - 1),
                 )
-            qT_of[i] = qT
 
         def transpose_s(i):
             sT = psum_s.tile([P, WORDS_PER_PASS, PASSES, P], F32)
@@ -162,49 +142,40 @@ def tile_capsulenetwork_pc_s_kernel(tc, s, Wc, bc, out):
                     )
             sT_of[i] = sT
 
-        def guesses(i):
-            qT = qT_of[i]
-            inv_root = per_tile.tile([P, P], F32)
-            nc.scalar.activation(out=inv_root[:], in_=qT[:], func=ACT.Abs_reciprocal_sqrt, bias=one_col)
-            inv_len = per_tile.tile([P, P], F32)
-            nc.scalar.activation(out=inv_len[:], in_=qT[:], func=ACT.Abs_reciprocal_sqrt, bias=eps_col)
-            inv_1q = per_tile.tile([P, P], F32)
-            nc.scalar.activation(out=inv_1q[:], in_=inv_root[:], func=ACT.Square, scale=H_SCALE_ROOT)
-            q = per_tile.tile([P, P], F32)
-            nc.scalar.copy(out=q[:], in_=qT[:])
-            inv_len_of[i], inv_1q_of[i], q_of[i] = inv_len, inv_1q, q
+        def logs(grp):
+            q = q_of[grp][:].rearrange("p i b -> p (i b)")
+            ln_1q = per_group.tile([P, GROUP * P], F32)
+            nc.scalar.activation(out=ln_1q[:], in_=q, func=ACT.Ln, bias=one_col)
+            ln_q = per_group.tile([P, GROUP * P], F32)
+            nc.scalar.activation(out=ln_q[:], in_=q, func=ACT.Ln, bias=eps_col)
+            return ln_1q, ln_q
 
-        def products(i):
-            eng = nc.vector if i < HEAD_TILES else nc.gpsimd
-            h = per_tile.tile([P, P], F32)
-            eng.tensor_tensor(out=h[:], in0=inv_len_of[i][:], in1=inv_1q_of[i][:], op=ALU.mult)
-            qh = per_tile.tile([P, P], F32)
-            eng.tensor_tensor(out=qh[:], in0=q_of[i][:], in1=h[:], op=ALU.mult)
-            ph = per_tile.tile([P, P], F32)
-            eng.tensor_tensor(out=ph[:], in0=qh[:], in1=h[:], op=ALU.add)
-            h_of[i], qh_of[i], ph_of[i] = h, qh, ph
-
-        def residual_square(i):
-            ph_sq = per_tile.tile([P, P], F32)
-            nc.scalar.activation(out=ph_sq[:], in_=ph_of[i][:], func=ACT.Square, scale=1.0 / H_SCALE)
-            ph_sq_of[i] = ph_sq
-            qh_true = per_tile.tile([P, P], F32)
-            nc.scalar.mul(out=qh_true[:], in_=qh_of[i][:], mul=NEWTON_SCALE / H_SCALE)
-            qh_true_of[i] = qh_true
-
-        def residual(i):
-            x = per_tile.tile([P, P], F32)
+        def join_logs(grp, pair):
+            ln_1q, ln_q = pair
+            m = per_group.tile([P, GROUP, P], F32)
             nc.vector.scalar_tensor_tensor(
-                out=x[:], in0=q_of[i][:], scalar=SQ_EPS, in1=ph_sq_of[i][:], op0=ALU.add, op1=ALU.mult
+                out=m[:].rearrange("p i b -> p (i b)"), in0=ln_q[:], scalar=0.5, in1=ln_1q[:], op0=ALU.mult, op1=ALU.add
             )
-            x_of[i] = x
+            m_of[grp] = m
 
-        def newton(i):
-            f = per_tile.tile([P, P], F32)
-            nc.vector.scalar_tensor_tensor(
-                out=f[:], in0=x_of[i][:], scalar=-NEWTON_SHIFT, in1=qh_true_of[i][:], op0=ALU.add, op1=ALU.mult
+        def exps(grp, slots):
+            if slots.start == 0:
+                e_of[grp] = per_group.tile([P, GROUP, P], F32, name="e")
+            nc.scalar.activation(
+                out=e_of[grp][:, slots, :], in_=m_of[grp][:, slots, :], func=ACT.Exp, scale=-1.0, bias=shift_col
             )
-            f_of[i] = f
+
+        def factor(grp, slots):
+            if slots.start == 0:
+                f_of[grp] = per_group.tile([P, GROUP, P], F32, name="f")
+            nc.vector.scalar_tensor_tensor(
+                out=f_of[grp][:, slots, :],
+                in0=q_of[grp][:, slots, :],
+                scalar=math.exp(-SHIFT),
+                in1=e_of[grp][:, slots, :],
+                op0=ALU.mult,
+                op1=ALU.mult,
+            )
 
         def multiply(i):
             shape = [P, P, WORDS_PER_PASS, WORD]
@@ -213,12 +184,12 @@ def tile_capsulenetwork_pc_s_kernel(tc, s, Wc, bc, out):
                 nc.vector.tensor_tensor(
                     out=v[:, g, :, :].rearrange("p b (u e) -> p b u e", e=WORD),
                     in0=sT_of[i][:, :, g, :].bitcast(BF16).rearrange("p u (b e) -> p b u e", e=WORD),
-                    in1=f_of[i][:].unsqueeze(2).unsqueeze(3).to_broadcast(shape),
+                    in1=f_of[i // GROUP][:, i % GROUP, :].unsqueeze(2).unsqueeze(3).to_broadcast(shape),
                     op=ALU.mult,
                 )
             v_of[i] = v
 
-        def quantise_and_matmul(i):
+        def quantise(i):
             v_codes = per_tile.tile([P, PASSES * P], U32, align_bytes=MX_ALIGN)
             v_scales = per_tile.tile([P, PASSES * P], U8, align_bytes=MX_ALIGN)
             nc.vector.quantize_mx(
@@ -245,42 +216,55 @@ def tile_capsulenetwork_pc_s_kernel(tc, s, Wc, bc, out):
             nc.vector.tensor_tensor(out=result[:], in0=acc_of[i][:], in1=bias[:], op=ALU.add)
             nc.sync.dma_start(out=out_rows[i], in_=result[:])
 
-        def is_tile(i):
-            return 0 <= i < B_TILES
-
-        for i in range(LEAD):
+        first, rest = slice(0, 1), slice(1, GROUP)
+        for i in range(3):
             square(i)
             sum_squares(i)
-        for i in range(LEAD):
+        for i in range(3):
             order_words(i)
-        for i in range(2):
+        transpose_s(0)
+        for i in range(3, 6):
+            square(i)
+            sum_squares(i)
+        for i in range(3, 5):
+            order_words(i)
+        pair = logs(0)
+        join_logs(0, pair)
+        order_words(5)
+        nc.vector.quantize_mx(
+            out=w_codes[:].rearrange("p g n -> p (g n)").bitcast(FP8X4),
+            scales=w_scales[:].rearrange("p g n -> p (g n)"),
+            in_=w_grouped[:].rearrange("p g n t -> p (g n t)"),
+        )
+        for i in range(1, 4):
             transpose_s(i)
-        group_weights()
-        for i in range(2):
-            guesses(i)
-            products(i)
-
-        for step in range(B_TILES + 2):
-            if is_tile(step):
-                residual_square(step)
-            if is_tile(step - 1):
-                multiply(step - 1)
-            if is_tile(step):
-                residual(step)
-            if step == 1:
-                quantise_weights()
-            if is_tile(step - 1):
-                quantise_and_matmul(step - 1)
-            if is_tile(step):
-                newton(step)
-            if is_tile(step - 2):
-                add_bias_and_store(step - 2)
-            if step >= 1 and is_tile(step + 1):
-                transpose_s(step + 1)
-            if is_tile(step + LEAD):
-                square(step + LEAD)
-                sum_squares(step + LEAD)
-                order_words(step + LEAD)
-            if is_tile(step + 2):
-                guesses(step + 2)
-                products(step + 2)
+        exps(0, first)
+        exps(0, rest)
+        pair = logs(1)
+        factor(0, first)
+        multiply(0)
+        transpose_s(4)
+        factor(0, rest)
+        multiply(1)
+        transpose_s(5)
+        quantise(0)
+        join_logs(1, pair)
+        exps(1, first)
+        exps(1, rest)
+        multiply(2)
+        quantise(1)
+        add_bias_and_store(0)
+        factor(1, first)
+        quantise(2)
+        add_bias_and_store(1)
+        multiply(3)
+        factor(1, rest)
+        quantise(3)
+        multiply(4)
+        add_bias_and_store(2)
+        quantise(4)
+        multiply(5)
+        add_bias_and_store(3)
+        quantise(5)
+        add_bias_and_store(4)
+        add_bias_and_store(5)

@@ -34,6 +34,7 @@ N_A, N_HALF, N_Z = 2, 2, 32
 SHIFT = 48.0
 
 GROUP = 3
+WARM_UPS = 4
 S_BANKS = 4
 Q_BANKS = 2
 OUT_BANKS = 2
@@ -66,6 +67,10 @@ def tile_capsulenetwork_pc_s_kernel(tc, s, Wc, bc, out):
         nc.scalar.activation(out=table_warm[:], in_=one_col, func=ACT.Ln)
         ident = keep.tile([P, P], F32)
         make_identity(nc, ident[:])
+
+        warm = psum_o.tile([P, N_OUT], F32, name="acc")
+        for i in range(WARM_UPS):
+            nc.tensor.matmul(out=warm[:], lhsT=ident[:], rhs=ident[:], start=True, stop=True)
 
         s_tiles = []
         for i in range(B_TILES):
@@ -197,7 +202,7 @@ def tile_capsulenetwork_pc_s_kernel(tc, s, Wc, bc, out):
                 scales=v_scales[:],
                 in_=v_of[i][:].rearrange("p g b t -> p (g b t)"),
             )
-            acc = psum_o.tile([P, N_OUT], F32)
+            acc = psum_o.tile([P, N_OUT], F32, name="acc")
             for g in range(PASSES):
                 rows = slice(g * P, (g + 1) * P)
                 nc.tensor.matmul_mx(

@@ -33,6 +33,9 @@ N_A, N_HALF, N_Z = 2, 2, 32
 
 SHIFT = 48.0
 
+TINY = 2.0**-60
+
+GPSIMD_WORDS = (3, 5)
 GROUP = 3
 WARM_UPS = 4
 S_BANKS = 4
@@ -56,10 +59,12 @@ def tile_capsulenetwork_pc_s_kernel(tc, s, Wc, bc, out):
         psum_q = ctx.enter_context(tc.psum_pool(name="psum_q", bufs=Q_BANKS))
         psum_o = ctx.enter_context(tc.psum_pool(name="psum_o", bufs=OUT_BANKS))
 
-        const_cols = keep.tile([P, 3], F32)
+        const_cols = keep.tile([P, 4], F32)
         nc.vector.memset(const_cols[:, 0:1], SQ_EPS)
         nc.vector.memset(const_cols[:, 1:2], 1.0)
         nc.vector.memset(const_cols[:, 2:3], SHIFT)
+        nc.vector.memset(const_cols[:, 3:4], TINY)
+        tiny_col = const_cols[:, 3:4]
         eps_col = const_cols[:, 0:1]
         one_col = const_cols[:, 1:2]
         shift_col = const_cols[:, 2:3]
@@ -91,36 +96,43 @@ def tile_capsulenetwork_pc_s_kernel(tc, s, Wc, bc, out):
         w_codes = keep.tile([P, PASSES, N_OUT], U32, align_bytes=MX_ALIGN)
         w_scales = keep.tile([P, PASSES, N_OUT], U8, align_bytes=MX_ALIGN)
         w_grouped = keep.tile([P, PASSES, N_OUT, PACK], BF16, align_bytes=MX_ALIGN)
-        nc.gpsimd.tensor_scalar(
-            out=w_grouped[:],
-            in0=w_raw[:].rearrange("p (g t) n -> p g n t", t=PACK),
-            scalar1=1.0,
-            scalar2=0.0,
-            op0=ALU.mult,
-            op1=ALU.add,
-        )
-
         words_of, squares_of, q_of, m_of, e_of, f_of = {}, {}, {}, {}, {}, {}
         sT_of, v_of, acc_of = {}, {}, {}
 
         def order_words(i):
             words = per_tile.tile([P, CAPS, CAP_WORDS], F32)
-            nc.vector.tensor_copy(
-                out=words[:].rearrange("b (A z a) w -> b A z a w", A=N_A, z=N_Z),
-                in_=s_tiles[i][:].bitcast(F32).rearrange(
-                    "b (A a z w) -> b A z a w", A=N_A, a=N_HALF, z=N_Z
-                ),
-            )
+            if i not in GPSIMD_WORDS:
+                nc.vector.tensor_copy(
+                    out=words[:].rearrange("b (A z a) w -> b A z a w", A=N_A, z=N_Z),
+                    in_=s_tiles[i][:].bitcast(F32).rearrange(
+                        "b (A a z w) -> b A z a w", A=N_A, a=N_HALF, z=N_Z
+                    ),
+                )
+            else:
+                for a in range(N_HALF):
+                    nc.gpsimd.tensor_scalar(
+                        out=words[:].rearrange("b c w -> b (c w)").bitcast(BF16).rearrange(
+                            "b (A z a o) -> b a A z o", A=N_A, z=N_Z, a=N_HALF
+                        )[:, a],
+                        in0=s_tiles[i][:].rearrange("b (A a z o) -> b a A z o", A=N_A, a=N_HALF, z=N_Z)[:, a],
+                        scalar1=1.0,
+                        scalar2=0.0,
+                        op0=ALU.mult,
+                        op1=ALU.add,
+                    )
             words_of[i] = words
 
-        def square(i):
+        def square(i, shared):
             squares = per_tile.tile([P, CAPS, CAP_LEN], F32)
             as_it_came = s_tiles[i][:].rearrange("b (A a z o) -> b a A z o", A=N_A, a=N_HALF, z=N_Z)
             ordered = squares[:].rearrange("b (A z a) o -> b a A z o", A=N_A, z=N_Z)
             nc.scalar.activation(out=ordered[:, 0], in_=as_it_came[:, 0], func=ACT.Square)
-            nc.vector.tensor_tensor(
-                out=ordered[:, 1], in0=as_it_came[:, 1], in1=as_it_came[:, 1], op=ALU.mult
-            )
+            if shared:
+                nc.vector.tensor_tensor(
+                    out=ordered[:, 1], in0=as_it_came[:, 1], in1=as_it_came[:, 1], op=ALU.mult
+                )
+            else:
+                nc.scalar.activation(out=ordered[:, 1], in_=as_it_came[:, 1], func=ACT.Square)
             squares_of[i] = squares
 
         def sum_squares(i):
@@ -137,6 +149,12 @@ def tile_capsulenetwork_pc_s_kernel(tc, s, Wc, bc, out):
                     start=(o == 0),
                     stop=(o == CAP_LEN - 1),
                 )
+
+        def reduce_squares(i):
+            q_row = keep.tile([P, CAPS], F32)
+            nc.vector.tensor_reduce(out=q_row[:], in_=squares_of[i][:], axis=mybir.AxisListType.X, op=ALU.add)
+            grp, slot = divmod(i, GROUP)
+            nc.tensor.transpose(q_of[grp][:, slot, :], q_row[:], ident[:])
 
         def transpose_s(i):
             sT = psum_s.tile([P, WORDS_PER_PASS, PASSES, P], F32)
@@ -162,6 +180,35 @@ def tile_capsulenetwork_pc_s_kernel(tc, s, Wc, bc, out):
                 out=m[:].rearrange("p i b -> p (i b)"), in0=ln_q[:], scalar=0.5, in1=ln_1q[:], op0=ALU.mult, op1=ALU.add
             )
             m_of[grp] = m
+
+        def logs_joined_by_gpsimd(grp, parts):
+            q = q_of[grp][:]
+            ln_len = per_group.tile([P, GROUP, P], F32)
+            nc.scalar.activation(out=ln_len[:], in_=q, func=ACT.Ln, bias=eps_col)
+            half = per_group.tile([P, GROUP, P], F32)
+            for slots in parts:
+                nc.gpsimd.tensor_scalar(
+                    out=half[:, slots, :], in0=ln_len[:, slots, :], scalar1=-0.5, scalar2=0.0, op0=ALU.mult, op1=ALU.add
+                )
+            ln_q = per_group.tile([P, GROUP, P], F32)
+            nc.scalar.activation(out=ln_q[:], in_=q, func=ACT.Ln, bias=tiny_col)
+            ln_1q = per_group.tile([P, GROUP, P], F32)
+            nc.scalar.activation(out=ln_1q[:], in_=q, func=ACT.Ln, bias=one_col)
+            top = per_group.tile([P, GROUP, P], F32)
+            m = per_group.tile([P, GROUP, P], F32)
+            for slots in parts:
+                nc.gpsimd.tensor_tensor(
+                    out=top[:, slots, :], in0=ln_q[:, slots, :], in1=half[:, slots, :], op=ALU.add
+                )
+                nc.gpsimd.tensor_tensor(
+                    out=m[:, slots, :], in0=top[:, slots, :], in1=ln_1q[:, slots, :], op=ALU.subtract
+                )
+            m_of[grp] = m
+
+        def exps_of_all(grp, slots):
+            if slots.start == 0:
+                f_of[grp] = per_group.tile([P, GROUP, P], F32, name="f")
+            nc.scalar.activation(out=f_of[grp][:, slots, :], in_=m_of[grp][:, slots, :], func=ACT.Exp)
 
         def exps(grp, slots):
             if slots.start == 0:
@@ -218,23 +265,38 @@ def tile_capsulenetwork_pc_s_kernel(tc, s, Wc, bc, out):
 
         def add_bias_and_store(i):
             result = per_tile.tile([P, N_OUT], F32)
-            nc.vector.tensor_tensor(out=result[:], in0=acc_of[i][:], in1=bias[:], op=ALU.add)
+            if i < 4:
+                plain = per_tile.tile([P, N_OUT], F32)
+                nc.scalar.copy(out=plain[:], in_=acc_of[i][:])
+                nc.gpsimd.tensor_tensor(out=result[:], in0=plain[:], in1=bias[:], op=ALU.add)
+            else:
+                nc.vector.tensor_tensor(out=result[:], in0=acc_of[i][:], in1=bias[:], op=ALU.add)
             nc.sync.dma_start(out=out_rows[i], in_=result[:])
 
         first, rest = slice(0, 1), slice(1, GROUP)
         for i in range(3):
-            square(i)
+            square(i, True)
+        for i in range(2):
             sum_squares(i)
+        reduce_squares(2)
         for i in range(3):
             order_words(i)
         transpose_s(0)
         for i in range(3, 6):
-            square(i)
+            square(i, i > 3)
             sum_squares(i)
-        for i in range(3, 5):
-            order_words(i)
+        order_words(3)
+        nc.gpsimd.tensor_scalar(
+            out=w_grouped[:],
+            in0=w_raw[:].rearrange("p (g t) n -> p g n t", t=PACK),
+            scalar1=1.0,
+            scalar2=0.0,
+            op0=ALU.mult,
+            op1=ALU.add,
+        )
         pair = logs(0)
         join_logs(0, pair)
+        order_words(4)
         order_words(5)
         nc.vector.quantize_mx(
             out=w_codes[:].rearrange("p g n -> p (g n)").bitcast(FP8X4),
@@ -245,7 +307,7 @@ def tile_capsulenetwork_pc_s_kernel(tc, s, Wc, bc, out):
             transpose_s(i)
         exps(0, first)
         exps(0, rest)
-        pair = logs(1)
+        logs_joined_by_gpsimd(1, (first, rest))
         factor(0, first)
         multiply(0)
         transpose_s(4)
@@ -253,22 +315,19 @@ def tile_capsulenetwork_pc_s_kernel(tc, s, Wc, bc, out):
         multiply(1)
         transpose_s(5)
         quantise(0)
-        join_logs(1, pair)
-        exps(1, first)
-        exps(1, rest)
+        exps_of_all(1, first)
+        exps_of_all(1, rest)
         multiply(2)
         quantise(1)
         add_bias_and_store(0)
-        factor(1, first)
+        multiply(3)
         quantise(2)
         add_bias_and_store(1)
-        multiply(3)
-        factor(1, rest)
-        quantise(3)
         multiply(4)
+        quantise(3)
         add_bias_and_store(2)
-        quantise(4)
         multiply(5)
+        quantise(4)
         add_bias_and_store(3)
         quantise(5)
         add_bias_and_store(4)

@@ -1,4 +1,3 @@
-import math
 from contextlib import ExitStack
 
 import concourse.mybir as mybir
@@ -31,15 +30,13 @@ WORDS_PER_PASS = PACK // WORD
 
 N_A, N_HALF, N_Z = 2, 2, 32
 
-SHIFT = 48.0
 
 TINY = 2.0**-60
 
-GPSIMD_WORDS = (3, 5)
 GROUP = 3
+BANK_TILES = 4
 WARM_UPS = 4
-S_BANKS = 4
-Q_BANKS = 2
+S_BANKS = 3
 OUT_BANKS = 2
 
 FLOPS = 2 * BATCH * K_TOTAL * N_OUT
@@ -56,18 +53,16 @@ def tile_capsulenetwork_pc_s_kernel(tc, s, Wc, bc, out):
         per_tile = ctx.enter_context(tc.tile_pool(name="per_tile", bufs=B_TILES))
         per_group = ctx.enter_context(tc.tile_pool(name="per_group", bufs=B_TILES // GROUP))
         psum_s = ctx.enter_context(tc.psum_pool(name="psum_s", bufs=S_BANKS))
-        psum_q = ctx.enter_context(tc.psum_pool(name="psum_q", bufs=Q_BANKS))
+        psum_q = ctx.enter_context(tc.psum_pool(name="psum_q", bufs=1))
         psum_o = ctx.enter_context(tc.psum_pool(name="psum_o", bufs=OUT_BANKS))
 
-        const_cols = keep.tile([P, 4], F32)
+        const_cols = keep.tile([P, 3], F32)
         nc.vector.memset(const_cols[:, 0:1], SQ_EPS)
         nc.vector.memset(const_cols[:, 1:2], 1.0)
-        nc.vector.memset(const_cols[:, 2:3], SHIFT)
-        nc.vector.memset(const_cols[:, 3:4], TINY)
-        tiny_col = const_cols[:, 3:4]
+        nc.vector.memset(const_cols[:, 2:3], TINY)
+        tiny_col = const_cols[:, 2:3]
         eps_col = const_cols[:, 0:1]
         one_col = const_cols[:, 1:2]
-        shift_col = const_cols[:, 2:3]
         table_warm = keep.tile([P, 1], F32)
         nc.scalar.activation(out=table_warm[:], in_=one_col, func=ACT.Ln)
         ident = keep.tile([P, P], F32)
@@ -96,53 +91,49 @@ def tile_capsulenetwork_pc_s_kernel(tc, s, Wc, bc, out):
         w_codes = keep.tile([P, PASSES, N_OUT], U32, align_bytes=MX_ALIGN)
         w_scales = keep.tile([P, PASSES, N_OUT], U8, align_bytes=MX_ALIGN)
         w_grouped = keep.tile([P, PASSES, N_OUT, PACK], BF16, align_bytes=MX_ALIGN)
-        words_of, squares_of, q_of, m_of, e_of, f_of = {}, {}, {}, {}, {}, {}
+        words_of, squares_of, m_of, top_of, f_of = {}, {}, {}, {}, {}
         sT_of, v_of, acc_of = {}, {}, {}
 
         def order_words(i):
             words = per_tile.tile([P, CAPS, CAP_WORDS], F32)
-            if i not in GPSIMD_WORDS:
-                nc.vector.tensor_copy(
-                    out=words[:].rearrange("b (A z a) w -> b A z a w", A=N_A, z=N_Z),
-                    in_=s_tiles[i][:].bitcast(F32).rearrange(
-                        "b (A a z w) -> b A z a w", A=N_A, a=N_HALF, z=N_Z
-                    ),
-                )
-            else:
-                for a in range(N_HALF):
-                    nc.gpsimd.tensor_scalar(
-                        out=words[:].rearrange("b c w -> b (c w)").bitcast(BF16).rearrange(
-                            "b (A z a o) -> b a A z o", A=N_A, z=N_Z, a=N_HALF
-                        )[:, a],
-                        in0=s_tiles[i][:].rearrange("b (A a z o) -> b a A z o", A=N_A, a=N_HALF, z=N_Z)[:, a],
-                        scalar1=1.0,
-                        scalar2=0.0,
-                        op0=ALU.mult,
-                        op1=ALU.add,
-                    )
+            nc.vector.tensor_copy(
+                out=words[:].rearrange("b (A z a) w -> b A z a w", A=N_A, z=N_Z),
+                in_=s_tiles[i][:].bitcast(F32).rearrange(
+                    "b (A a z w) -> b A z a w", A=N_A, a=N_HALF, z=N_Z
+                ),
+            )
             words_of[i] = words
 
-        def square(i, shared):
+        def square(i):
             squares = per_tile.tile([P, CAPS, CAP_LEN], F32)
             as_it_came = s_tiles[i][:].rearrange("b (A a z o) -> b a A z o", A=N_A, a=N_HALF, z=N_Z)
             ordered = squares[:].rearrange("b (A z a) o -> b a A z o", A=N_A, z=N_Z)
             nc.scalar.activation(out=ordered[:, 0], in_=as_it_came[:, 0], func=ACT.Square)
-            if shared:
+            if i == 3:
+                nc.scalar.activation(out=ordered[:, 1], in_=as_it_came[:, 1], func=ACT.Square)
+            else:
                 nc.vector.tensor_tensor(
                     out=ordered[:, 1], in0=as_it_came[:, 1], in1=as_it_came[:, 1], op=ALU.mult
                 )
-            else:
-                nc.scalar.activation(out=ordered[:, 1], in_=as_it_came[:, 1], func=ACT.Square)
             squares_of[i] = squares
 
-        def sum_squares(i):
+        q_head = psum_q.tile([P, BANK_TILES, P], F32)
+        q_rest = psum_q.tile([P, BANK_TILES, P], F32)
+        q_next = psum_q.tile([P, BANK_TILES, P], F32)
+
+        def q_slots(grp, slots):
+            if grp == 1:
+                return q_next[:, slots, :]
+            return q_head[:, slots, :] if slots.start == 0 else q_rest[:, slots, :]
+
+        def q_slot(i):
             grp, slot = divmod(i, GROUP)
-            if slot == 0:
-                q_bank = psum_q.tile([P, GROUP, P], F32)
-                q_of[grp] = q_bank
+            return q_slots(grp, slice(slot, slot + 1))[:, 0, :]
+
+        def sum_squares(i):
             for o in range(CAP_LEN):
                 nc.tensor.matmul(
-                    out=q_of[grp][:, slot, :],
+                    out=q_slot(i),
                     lhsT=squares_of[i][:, :, o],
                     rhs=ident[:],
                     is_transpose=True,
@@ -153,8 +144,7 @@ def tile_capsulenetwork_pc_s_kernel(tc, s, Wc, bc, out):
         def reduce_squares(i):
             q_row = keep.tile([P, CAPS], F32)
             nc.vector.tensor_reduce(out=q_row[:], in_=squares_of[i][:], axis=mybir.AxisListType.X, op=ALU.add)
-            grp, slot = divmod(i, GROUP)
-            nc.tensor.transpose(q_of[grp][:, slot, :], q_row[:], ident[:])
+            nc.tensor.transpose(q_slot(i), q_row[:], ident[:])
 
         def transpose_s(i):
             sT = psum_s.tile([P, WORDS_PER_PASS, PASSES, P], F32)
@@ -165,69 +155,33 @@ def tile_capsulenetwork_pc_s_kernel(tc, s, Wc, bc, out):
                     )
             sT_of[i] = sT
 
-        def logs(grp):
-            q = q_of[grp][:].rearrange("p i b -> p (i b)")
-            ln_1q = per_group.tile([P, GROUP * P], F32)
-            nc.scalar.activation(out=ln_1q[:], in_=q, func=ACT.Ln, bias=one_col)
-            ln_q = per_group.tile([P, GROUP * P], F32)
-            nc.scalar.activation(out=ln_q[:], in_=q, func=ACT.Ln, bias=eps_col)
-            return ln_1q, ln_q
+        def logs(grp, slots):
+            n = slots.stop - slots.start
+            found = []
+            for bias_col, name in ((eps_col, "ln_len"), (tiny_col, "ln_q"), (one_col, "ln_1q")):
+                ln = keep.tile([P, GROUP, P], F32, name="%s_%d_%d" % (name, grp, slots.start))
+                nc.scalar.activation(out=ln[:, :n, :], in_=q_slots(grp, slots), func=ACT.Ln, bias=bias_col)
+                found.append(ln[:, :n, :])
+            return found
 
-        def join_logs(grp, pair):
-            ln_1q, ln_q = pair
-            m = per_group.tile([P, GROUP, P], F32)
-            nc.vector.scalar_tensor_tensor(
-                out=m[:].rearrange("p i b -> p (i b)"), in0=ln_q[:], scalar=0.5, in1=ln_1q[:], op0=ALU.mult, op1=ALU.add
-            )
-            m_of[grp] = m
-
-        def logs_joined_by_gpsimd(grp, parts):
-            q = q_of[grp][:]
-            ln_len = per_group.tile([P, GROUP, P], F32)
-            nc.scalar.activation(out=ln_len[:], in_=q, func=ACT.Ln, bias=eps_col)
-            half = per_group.tile([P, GROUP, P], F32)
-            for slots in parts:
-                nc.gpsimd.tensor_scalar(
-                    out=half[:, slots, :], in0=ln_len[:, slots, :], scalar1=-0.5, scalar2=0.0, op0=ALU.mult, op1=ALU.add
-                )
-            ln_q = per_group.tile([P, GROUP, P], F32)
-            nc.scalar.activation(out=ln_q[:], in_=q, func=ACT.Ln, bias=tiny_col)
-            ln_1q = per_group.tile([P, GROUP, P], F32)
-            nc.scalar.activation(out=ln_1q[:], in_=q, func=ACT.Ln, bias=one_col)
-            top = per_group.tile([P, GROUP, P], F32)
-            m = per_group.tile([P, GROUP, P], F32)
-            for slots in parts:
-                nc.gpsimd.tensor_tensor(
-                    out=top[:, slots, :], in0=ln_q[:, slots, :], in1=half[:, slots, :], op=ALU.add
-                )
-                nc.gpsimd.tensor_tensor(
-                    out=m[:, slots, :], in0=top[:, slots, :], in1=ln_1q[:, slots, :], op=ALU.subtract
-                )
-            m_of[grp] = m
-
-        def exps_of_all(grp, slots):
+        def join_len(grp, slots, found):
             if slots.start == 0:
-                f_of[grp] = per_group.tile([P, GROUP, P], F32, name="f")
-            nc.scalar.activation(out=f_of[grp][:, slots, :], in_=m_of[grp][:, slots, :], func=ACT.Exp)
+                top_of[grp] = per_group.tile([P, GROUP, P], F32, name="top")
+            nc.vector.scalar_tensor_tensor(
+                out=top_of[grp][:, slots, :], in0=found[0], scalar=-0.5, in1=found[1], op0=ALU.mult, op1=ALU.add
+            )
+
+        def join_1q(grp, slots, found):
+            if slots.start == 0:
+                m_of[grp] = per_group.tile([P, GROUP, P], F32, name="m")
+            nc.vector.tensor_tensor(
+                out=m_of[grp][:, slots, :], in0=top_of[grp][:, slots, :], in1=found[2], op=ALU.subtract
+            )
 
         def exps(grp, slots):
             if slots.start == 0:
-                e_of[grp] = per_group.tile([P, GROUP, P], F32, name="e")
-            nc.scalar.activation(
-                out=e_of[grp][:, slots, :], in_=m_of[grp][:, slots, :], func=ACT.Exp, scale=-1.0, bias=shift_col
-            )
-
-        def factor(grp, slots):
-            if slots.start == 0:
                 f_of[grp] = per_group.tile([P, GROUP, P], F32, name="f")
-            nc.vector.scalar_tensor_tensor(
-                out=f_of[grp][:, slots, :],
-                in0=q_of[grp][:, slots, :],
-                scalar=math.exp(-SHIFT),
-                in1=e_of[grp][:, slots, :],
-                op0=ALU.mult,
-                op1=ALU.mult,
-            )
+            nc.scalar.activation(out=f_of[grp][:, slots, :], in_=m_of[grp][:, slots, :], func=ACT.Exp)
 
         def multiply(i):
             shape = [P, P, WORDS_PER_PASS, WORD]
@@ -263,29 +217,49 @@ def tile_capsulenetwork_pc_s_kernel(tc, s, Wc, bc, out):
                 )
             acc_of[i] = acc
 
+        def quantise_weights():
+            nc.vector.quantize_mx(
+                out=w_codes[:].rearrange("p g n -> p (g n)").bitcast(FP8X4),
+                scales=w_scales[:].rearrange("p g n -> p (g n)"),
+                in_=w_grouped[:].rearrange("p g n t -> p (g n t)"),
+            )
+
         def add_bias_and_store(i):
             result = per_tile.tile([P, N_OUT], F32)
-            if i < 4:
-                plain = per_tile.tile([P, N_OUT], F32)
-                nc.scalar.copy(out=plain[:], in_=acc_of[i][:])
-                nc.gpsimd.tensor_tensor(out=result[:], in0=plain[:], in1=bias[:], op=ALU.add)
-            else:
-                nc.vector.tensor_tensor(out=result[:], in0=acc_of[i][:], in1=bias[:], op=ALU.add)
+            nc.vector.tensor_tensor(out=result[:], in0=acc_of[i][:], in1=bias[:], op=ALU.add)
             nc.sync.dma_start(out=out_rows[i], in_=result[:])
 
-        first, rest = slice(0, 1), slice(1, GROUP)
+        first, rest, whole = slice(0, 1), slice(1, GROUP), slice(0, GROUP)
         for i in range(3):
-            square(i, True)
+            square(i)
         for i in range(2):
             sum_squares(i)
         reduce_squares(2)
-        for i in range(3):
-            order_words(i)
+        order_words(0)
         transpose_s(0)
-        for i in range(3, 6):
-            square(i, i > 3)
-            sum_squares(i)
+        square(3)
+        head_logs = logs(0, first)
+        square(4)
+        rest_logs = logs(0, rest)
+        order_words(1)
+        join_len(0, first, head_logs)
+        order_words(2)
+        join_1q(0, first, head_logs)
+        sum_squares(3)
+        transpose_s(1)
+        sum_squares(4)
+        transpose_s(2)
+        exps(0, first)
+        join_len(0, rest, rest_logs)
+        square(5)
+        sum_squares(5)
+        join_1q(0, rest, rest_logs)
+        exps(0, rest)
+        next_logs = logs(1, whole)
         order_words(3)
+        order_words(4)
+        turn = keep.tile([P, 1], F32)
+        nc.gpsimd.tensor_copy(out=turn[:], in_=f_of[0][:, 0, 0:1])
         nc.gpsimd.tensor_scalar(
             out=w_grouped[:],
             in0=w_raw[:].rearrange("p (g t) n -> p g n t", t=PACK),
@@ -294,34 +268,23 @@ def tile_capsulenetwork_pc_s_kernel(tc, s, Wc, bc, out):
             op0=ALU.mult,
             op1=ALU.add,
         )
-        pair = logs(0)
-        join_logs(0, pair)
-        order_words(4)
-        order_words(5)
-        nc.vector.quantize_mx(
-            out=w_codes[:].rearrange("p g n -> p (g n)").bitcast(FP8X4),
-            scales=w_scales[:].rearrange("p g n -> p (g n)"),
-            in_=w_grouped[:].rearrange("p g n t -> p (g n t)"),
-        )
-        for i in range(1, 4):
-            transpose_s(i)
-        exps(0, first)
-        exps(0, rest)
-        logs_joined_by_gpsimd(1, (first, rest))
-        factor(0, first)
         multiply(0)
-        transpose_s(4)
-        factor(0, rest)
+        transpose_s(3)
+        order_words(5)
         multiply(1)
-        transpose_s(5)
+        transpose_s(4)
+        quantise_weights()
         quantise(0)
-        exps_of_all(1, first)
-        exps_of_all(1, rest)
+        join_len(1, whole, next_logs)
         multiply(2)
+        join_1q(1, whole, next_logs)
+        exps(1, first)
+        exps(1, rest)
+        transpose_s(5)
         quantise(1)
         add_bias_and_store(0)
-        multiply(3)
         quantise(2)
+        multiply(3)
         add_bias_and_store(1)
         multiply(4)
         quantise(3)

@@ -92,7 +92,7 @@ def tile_capsulenetwork_pc_s_kernel(tc, s, Wc, bc, out):
         w_scales = keep.tile([P, PASSES, N_OUT], U8, align_bytes=MX_ALIGN)
         w_grouped = keep.tile([P, PASSES, N_OUT, PACK], BF16, align_bytes=MX_ALIGN)
         words_of, squares_of, m_of, top_of, f_of = {}, {}, {}, {}, {}
-        sT_of, v_of, acc_of = {}, {}, {}
+        sT_of, v_of, codes_of, scales_of, acc_of = {}, {}, {}, {}, {}
 
         def order_words(i):
             words = per_tile.tile([P, CAPS, CAP_WORDS], F32)
@@ -147,11 +147,11 @@ def tile_capsulenetwork_pc_s_kernel(tc, s, Wc, bc, out):
             nc.tensor.transpose(q_slot(i), q_row[:], ident[:])
 
         def transpose_s(i):
-            sT = psum_s.tile([P, WORDS_PER_PASS, PASSES, P], F32)
+            sT = psum_s.tile([P, PASSES, P, WORDS_PER_PASS], F32)
             for g in range(PASSES):
                 for u in range(WORDS_PER_PASS):
                     nc.tensor.transpose(
-                        sT[:, u, g, :], words_of[i][:, :, g * WORDS_PER_PASS + u], ident[:]
+                        sT[:, g, :, u], words_of[i][:, :, g * WORDS_PER_PASS + u], ident[:]
                     )
             sT_of[i] = sT
 
@@ -183,39 +183,39 @@ def tile_capsulenetwork_pc_s_kernel(tc, s, Wc, bc, out):
                 f_of[grp] = per_group.tile([P, GROUP, P], F32, name="f")
             nc.scalar.activation(out=f_of[grp][:, slots, :], in_=m_of[grp][:, slots, :], func=ACT.Exp)
 
-        def multiply(i):
-            shape = [P, P, WORDS_PER_PASS, WORD]
-            v = per_tile.tile([P, PASSES, P, PACK], BF16, align_bytes=MX_ALIGN)
-            for g in range(PASSES):
-                nc.vector.tensor_tensor(
-                    out=v[:, g, :, :].rearrange("p b (u e) -> p b u e", e=WORD),
-                    in0=sT_of[i][:, :, g, :].bitcast(BF16).rearrange("p u (b e) -> p b u e", e=WORD),
-                    in1=f_of[i // GROUP][:, i % GROUP, :].unsqueeze(2).unsqueeze(3).to_broadcast(shape),
-                    op=ALU.mult,
-                )
-            v_of[i] = v
-
-        def quantise(i):
-            v_codes = per_tile.tile([P, PASSES * P], U32, align_bytes=MX_ALIGN)
-            v_scales = per_tile.tile([P, PASSES * P], U8, align_bytes=MX_ALIGN)
-            nc.vector.quantize_mx(
-                out=v_codes[:].bitcast(FP8X4),
-                scales=v_scales[:],
-                in_=v_of[i][:].rearrange("p g b t -> p (g b t)"),
+        def multiply(i, passes):
+            if passes.start == 0:
+                v_of[i] = per_tile.tile([P, PASSES, P, PACK], BF16, align_bytes=MX_ALIGN, name="v")
+            shape = [P, passes.stop - passes.start, P, PACK]
+            nc.vector.tensor_tensor(
+                out=v_of[i][:, passes],
+                in0=sT_of[i][:, passes].rearrange("p g b u -> p g (b u)").bitcast(BF16).rearrange("p g (b t) -> p g b t", t=PACK),
+                in1=f_of[i // GROUP][:, i % GROUP, :].unsqueeze(1).unsqueeze(3).to_broadcast(shape),
+                op=ALU.mult,
             )
-            acc = psum_o.tile([P, N_OUT], F32, name="acc")
-            for g in range(PASSES):
+
+        def quantise(i, passes):
+            if passes.start == 0:
+                codes_of[i] = per_tile.tile([P, PASSES * P], U32, align_bytes=MX_ALIGN, name="v_codes")
+                scales_of[i] = per_tile.tile([P, PASSES * P], U8, align_bytes=MX_ALIGN, name="v_scales")
+                acc_of[i] = psum_o.tile([P, N_OUT], F32, name="acc")
+            cols = slice(passes.start * P, passes.stop * P)
+            nc.vector.quantize_mx(
+                out=codes_of[i][:, cols].bitcast(FP8X4),
+                scales=scales_of[i][:, cols],
+                in_=v_of[i][:, passes].rearrange("p g b t -> p (g b t)"),
+            )
+            for g in range(passes.start, passes.stop):
                 rows = slice(g * P, (g + 1) * P)
                 nc.tensor.matmul_mx(
-                    out=acc[:],
-                    lhsT=v_codes[:, rows].bitcast(FP8X4),
-                    lhsT_scale=v_scales[:, rows],
+                    out=acc_of[i][:],
+                    lhsT=codes_of[i][:, rows].bitcast(FP8X4),
+                    lhsT_scale=scales_of[i][:, rows],
                     rhs=w_codes[:, g, :].bitcast(FP8X4),
                     rhs_scale=w_scales[:, g, :],
                     start=(g == 0),
                     stop=(g == PASSES - 1),
                 )
-            acc_of[i] = acc
 
         def quantise_weights():
             nc.vector.quantize_mx(
@@ -226,7 +226,12 @@ def tile_capsulenetwork_pc_s_kernel(tc, s, Wc, bc, out):
 
         def add_bias_and_store(i):
             result = per_tile.tile([P, N_OUT], F32)
-            nc.vector.tensor_tensor(out=result[:], in0=acc_of[i][:], in1=bias[:], op=ALU.add)
+            if i < 4:
+                plain = per_tile.tile([P, N_OUT], F32)
+                nc.scalar.copy(out=plain[:], in_=acc_of[i][:])
+                nc.gpsimd.tensor_tensor(out=result[:], in0=plain[:], in1=bias[:], op=ALU.add)
+            else:
+                nc.vector.tensor_tensor(out=result[:], in0=acc_of[i][:], in1=bias[:], op=ALU.add)
             nc.sync.dma_start(out=out_rows[i], in_=result[:])
 
         first, rest, whole = slice(0, 1), slice(1, GROUP), slice(0, GROUP)
@@ -268,30 +273,33 @@ def tile_capsulenetwork_pc_s_kernel(tc, s, Wc, bc, out):
             op0=ALU.mult,
             op1=ALU.add,
         )
-        multiply(0)
+        both, low, high = slice(0, PASSES), slice(0, 1), slice(1, PASSES)
+        multiply(0, both)
         transpose_s(3)
         order_words(5)
-        multiply(1)
+        multiply(1, both)
         transpose_s(4)
         quantise_weights()
-        quantise(0)
+        quantise(0, both)
         join_len(1, whole, next_logs)
-        multiply(2)
+        multiply(2, both)
         join_1q(1, whole, next_logs)
         exps(1, first)
         exps(1, rest)
         transpose_s(5)
-        quantise(1)
+        quantise(1, both)
         add_bias_and_store(0)
-        quantise(2)
-        multiply(3)
+        quantise(2, both)
         add_bias_and_store(1)
-        multiply(4)
-        quantise(3)
+        multiply(3, both)
         add_bias_and_store(2)
-        multiply(5)
-        quantise(4)
+        multiply(4, both)
+        quantise(3, both)
         add_bias_and_store(3)
-        quantise(5)
+        multiply(5, low)
+        quantise(4, both)
+        multiply(5, high)
+        quantise(5, low)
+        quantise(5, high)
         add_bias_and_store(4)
         add_bias_and_store(5)

@@ -276,9 +276,9 @@ def tile_capsulenetwork_pc_s_kernel(tc, s, Wc, bc, out):
         both, low, high = slice(0, PASSES), slice(0, 1), slice(1, PASSES)
         multiply(0, both)
         transpose_s(3)
-        order_words(5)
         multiply(1, both)
         transpose_s(4)
+        order_words(5)
         quantise_weights()
         quantise(0, both)
         join_len(1, whole, next_logs)

from contextlib import ExitStack

import concourse.mybir as mybir
from concourse.masks import make_identity

F32 = mybir.dt.float32
BF16 = mybir.dt.bfloat16
U32 = mybir.dt.uint32
U8 = mybir.dt.uint8
FP8X4 = mybir.dt.float8_e4m3fn_x4
ACT = mybir.ActivationFunctionType
ALU = mybir.AluOpType

P = 128
MX_ALIGN = 64
PACK = 4

BATCH = 768
CAPS = 128
CAP_LEN = 8
K_TOTAL = CAPS * CAP_LEN
N_OUT = 128
SQ_EPS = 1e-8

B_TILES = BATCH // P
PASSES = CAP_LEN // PACK
WORD = 2
CAP_WORDS = CAP_LEN // WORD
WORDS_PER_PASS = PACK // WORD

N_A, N_HALF, N_Z = 2, 2, 32


TINY = 2.0**-60

GROUP = 3
BANK_TILES = 4
WARM_UPS = 4
S_BANKS = 3
OUT_BANKS = 2

FLOPS = 2 * BATCH * K_TOTAL * N_OUT


def tile_capsulenetwork_pc_s_kernel(tc, s, Wc, bc, out):
    nc = tc.nc
    s_rows = s.rearrange("(i b) j o -> i b (j o)", b=P)
    out_rows = out.rearrange("(i b) n -> i b n", b=P)

    with ExitStack() as ctx:
        ctx.enter_context(tc.manual_schedule())
        keep = ctx.enter_context(tc.tile_pool(name="keep", bufs=1))
        per_tile = ctx.enter_context(tc.tile_pool(name="per_tile", bufs=B_TILES))
        per_group = ctx.enter_context(tc.tile_pool(name="per_group", bufs=B_TILES // GROUP))
        psum_s = ctx.enter_context(tc.psum_pool(name="psum_s", bufs=S_BANKS))
        psum_q = ctx.enter_context(tc.psum_pool(name="psum_q", bufs=1))
        psum_o = ctx.enter_context(tc.psum_pool(name="psum_o", bufs=OUT_BANKS))

        const_cols = keep.tile([P, 3], F32)
        nc.vector.memset(const_cols[:, 0:1], SQ_EPS)
        nc.vector.memset(const_cols[:, 1:2], 1.0)
        nc.vector.memset(const_cols[:, 2:3], TINY)
        tiny_col = const_cols[:, 2:3]
        eps_col = const_cols[:, 0:1]
        one_col = const_cols[:, 1:2]
        table_warm = keep.tile([P, 1], F32)
        nc.scalar.activation(out=table_warm[:], in_=one_col, func=ACT.Ln)
        ident = keep.tile([P, P], F32)
        make_identity(nc, ident[:])

        warm = psum_o.tile([P, N_OUT], F32, name="acc")
        for i in range(WARM_UPS):
            nc.tensor.matmul(out=warm[:], lhsT=ident[:], rhs=ident[:], start=True, stop=True)

        s_tiles = []
        for i in range(B_TILES):
            s_tile = per_tile.tile([P, K_TOTAL], BF16)
            nc.sync.dma_start(out=s_tile[:], in_=s_rows[i])
            s_tiles.append(s_tile)
        w_raw = keep.tile([P, CAP_LEN, N_OUT], BF16)
        w_caps = Wc.rearrange("(c z o) n -> c z (o n)", z=N_Z, o=CAP_LEN)
        for c in range(N_A * N_HALF):
            first = (c // N_HALF) * (N_HALF * N_Z) + c % N_HALF
            nc.sync.dma_start(
                out=w_raw[first : first + N_HALF * (N_Z - 1) + 1 : N_HALF, :, :].rearrange("p o n -> p (o n)"),
                in_=w_caps[c],
            )
        bias = keep.tile([P, N_OUT], BF16)
        nc.sync.dma_start(out=bias[:], in_=bc.partition_broadcast(P))

        w_codes = keep.tile([P, PASSES, N_OUT], U32, align_bytes=MX_ALIGN)
        w_scales = keep.tile([P, PASSES, N_OUT], U8, align_bytes=MX_ALIGN)
        w_grouped = keep.tile([P, PASSES, N_OUT, PACK], BF16, align_bytes=MX_ALIGN)
        words_of, squares_of, m_of, top_of, f_of = {}, {}, {}, {}, {}
        sT_of, v_of, codes_of, scales_of, acc_of = {}, {}, {}, {}, {}

        def order_words(i):
            words = per_tile.tile([P, CAPS, CAP_WORDS], F32)
            nc.vector.tensor_copy(
                out=words[:].rearrange("b (A z a) w -> b A z a w", A=N_A, z=N_Z),
                in_=s_tiles[i][:].bitcast(F32).rearrange(
                    "b (A a z w) -> b A z a w", A=N_A, a=N_HALF, z=N_Z
                ),
            )
            words_of[i] = words

        def square(i):
            squares = per_tile.tile([P, CAPS, CAP_LEN], F32)
            as_it_came = s_tiles[i][:].rearrange("b (A a z o) -> b a A z o", A=N_A, a=N_HALF, z=N_Z)
            ordered = squares[:].rearrange("b (A z a) o -> b a A z o", A=N_A, z=N_Z)
            nc.scalar.activation(out=ordered[:, 0], in_=as_it_came[:, 0], func=ACT.Square)
            if i == 3:
                nc.scalar.activation(out=ordered[:, 1], in_=as_it_came[:, 1], func=ACT.Square)
            else:
                nc.vector.tensor_tensor(
                    out=ordered[:, 1], in0=as_it_came[:, 1], in1=as_it_came[:, 1], op=ALU.mult
                )
            squares_of[i] = squares

        q_head = psum_q.tile([P, BANK_TILES, P], F32)
        q_rest = psum_q.tile([P, BANK_TILES, P], F32)
        q_next = psum_q.tile([P, BANK_TILES, P], F32)

        def q_slots(grp, slots):
            if grp == 1:
                return q_next[:, slots, :]
            return q_head[:, slots, :] if slots.start == 0 else q_rest[:, slots, :]

        def q_slot(i):
            grp, slot = divmod(i, GROUP)
            return q_slots(grp, slice(slot, slot + 1))[:, 0, :]

        def sum_squares(i):
            for o in range(CAP_LEN):
                nc.tensor.matmul(
                    out=q_slot(i),
                    lhsT=squares_of[i][:, :, o],
                    rhs=ident[:],
                    is_transpose=True,
                    start=(o == 0),
                    stop=(o == CAP_LEN - 1),
                )

        def reduce_squares(i):
            q_row = keep.tile([P, CAPS], F32)
            nc.vector.tensor_reduce(out=q_row[:], in_=squares_of[i][:], axis=mybir.AxisListType.X, op=ALU.add)
            nc.tensor.transpose(q_slot(i), q_row[:], ident[:])

        def transpose_s(i):
            sT = psum_s.tile([P, PASSES, P, WORDS_PER_PASS], F32)
            for g in range(PASSES):
                for u in range(WORDS_PER_PASS):
                    nc.tensor.transpose(
                        sT[:, g, :, u], words_of[i][:, :, g * WORDS_PER_PASS + u], ident[:]
                    )
            sT_of[i] = sT

        def logs(grp, slots):
            n = slots.stop - slots.start
            found = []
            for bias_col, name in ((eps_col, "ln_len"), (tiny_col, "ln_q"), (one_col, "ln_1q")):
                ln = keep.tile([P, GROUP, P], F32, name="%s_%d_%d" % (name, grp, slots.start))
                nc.scalar.activation(out=ln[:, :n, :], in_=q_slots(grp, slots), func=ACT.Ln, bias=bias_col)
                found.append(ln[:, :n, :])
            return found

        def join_len(grp, slots, found):
            if slots.start == 0:
                top_of[grp] = per_group.tile([P, GROUP, P], F32, name="top")
            nc.vector.scalar_tensor_tensor(
                out=top_of[grp][:, slots, :], in0=found[0], scalar=-0.5, in1=found[1], op0=ALU.mult, op1=ALU.add
            )

        def join_1q(grp, slots, found):
            if slots.start == 0:
                m_of[grp] = per_group.tile([P, GROUP, P], F32, name="m")
            nc.vector.tensor_tensor(
                out=m_of[grp][:, slots, :], in0=top_of[grp][:, slots, :], in1=found[2], op=ALU.subtract
            )

        def exps(grp, slots):
            if slots.start == 0:
                f_of[grp] = per_group.tile([P, GROUP, P], F32, name="f")
            nc.scalar.activation(out=f_of[grp][:, slots, :], in_=m_of[grp][:, slots, :], func=ACT.Exp)

        def multiply(i, passes):
            if passes.start == 0:
                v_of[i] = per_tile.tile([P, PASSES, P, PACK], BF16, align_bytes=MX_ALIGN, name="v")
            shape = [P, passes.stop - passes.start, P, PACK]
            nc.vector.tensor_tensor(
                out=v_of[i][:, passes],
                in0=sT_of[i][:, passes].rearrange("p g b u -> p g (b u)").bitcast(BF16).rearrange("p g (b t) -> p g b t", t=PACK),
                in1=f_of[i // GROUP][:, i % GROUP, :].unsqueeze(1).unsqueeze(3).to_broadcast(shape),
                op=ALU.mult,
            )

        def quantise(i, passes):
            if passes.start == 0:
                codes_of[i] = per_tile.tile([P, PASSES * P], U32, align_bytes=MX_ALIGN, name="v_codes")
                scales_of[i] = per_tile.tile([P, PASSES * P], U8, align_bytes=MX_ALIGN, name="v_scales")
                acc_of[i] = psum_o.tile([P, N_OUT], F32, name="acc")
            cols = slice(passes.start * P, passes.stop * P)
            nc.vector.quantize_mx(
                out=codes_of[i][:, cols].bitcast(FP8X4),
                scales=scales_of[i][:, cols],
                in_=v_of[i][:, passes].rearrange("p g b t -> p (g b t)"),
            )
            for g in range(passes.start, passes.stop):
                rows = slice(g * P, (g + 1) * P)
                nc.tensor.matmul_mx(
                    out=acc_of[i][:],
                    lhsT=codes_of[i][:, rows].bitcast(FP8X4),
                    lhsT_scale=scales_of[i][:, rows],
                    rhs=w_codes[:, g, :].bitcast(FP8X4),
                    rhs_scale=w_scales[:, g, :],
                    start=(g == 0),
                    stop=(g == PASSES - 1),
                )

        def quantise_weights():
            nc.vector.quantize_mx(
                out=w_codes[:].rearrange("p g n -> p (g n)").bitcast(FP8X4),
                scales=w_scales[:].rearrange("p g n -> p (g n)"),
                in_=w_grouped[:].rearrange("p g n t -> p (g n t)"),
            )

        def add_bias_and_store(i):
            result = per_tile.tile([P, N_OUT], F32)
            if i < 4:
                plain = per_tile.tile([P, N_OUT], F32)
                nc.scalar.copy(out=plain[:], in_=acc_of[i][:])
                nc.gpsimd.tensor_tensor(out=result[:], in0=plain[:], in1=bias[:], op=ALU.add)
            else:
                nc.vector.tensor_tensor(out=result[:], in0=acc_of[i][:], in1=bias[:], op=ALU.add)
            nc.sync.dma_start(out=out_rows[i], in_=result[:])

        first, rest, whole = slice(0, 1), slice(1, GROUP), slice(0, GROUP)
        for i in range(3):
            square(i)
        for i in range(2):
            sum_squares(i)
        reduce_squares(2)
        order_words(0)
        transpose_s(0)
        square(3)
        head_logs = logs(0, first)
        square(4)
        rest_logs = logs(0, rest)
        order_words(1)
        join_len(0, first, head_logs)
        order_words(2)
        join_1q(0, first, head_logs)
        sum_squares(3)
        transpose_s(1)
        sum_squares(4)
        transpose_s(2)
        exps(0, first)
        join_len(0, rest, rest_logs)
        square(5)
        sum_squares(5)
        join_1q(0, rest, rest_logs)
        exps(0, rest)
        next_logs = logs(1, whole)
        order_words(3)
        order_words(4)
        turn = keep.tile([P, 1], F32)
        nc.gpsimd.tensor_copy(out=turn[:], in_=f_of[0][:, 0, 0:1])
        nc.gpsimd.tensor_scalar(
            out=w_grouped[:],
            in0=w_raw[:].rearrange("p (g t) n -> p g n t", t=PACK),
            scalar1=1.0,
            scalar2=0.0,
            op0=ALU.mult,
            op1=ALU.add,
        )
        both, low, high = slice(0, PASSES), slice(0, 1), slice(1, PASSES)
        multiply(0, both)
        transpose_s(3)
        multiply(1, both)
        transpose_s(4)
        order_words(5)
        quantise_weights()
        quantise(0, both)
        join_len(1, whole, next_logs)
        multiply(2, both)
        join_1q(1, whole, next_logs)
        exps(1, first)
        exps(1, rest)
        transpose_s(5)
        quantise(1, both)
        add_bias_and_store(0)
        quantise(2, both)
        add_bias_and_store(1)
        multiply(3, both)
        add_bias_and_store(2)
        multiply(4, both)
        quantise(3, both)
        add_bias_and_store(3)
        multiply(5, low)
        quantise(4, both)
        multiply(5, high)
        quantise(5, low)
        quantise(5, high)
        add_bias_and_store(4)
        add_bias_and_store(5)
